import numpy as np
import ml_dtypes


def mxq(x, axis, fmt="e4m3"):
    dtype, down = {"e4m3": (ml_dtypes.float8_e4m3fn, 7), "e5m2": (ml_dtypes.float8_e5m2, 14)}[fmt]
    v = np.moveaxis(np.asarray(x, np.float32).astype(ml_dtypes.bfloat16).astype(np.float64), axis, -1)
    blocks = v.reshape(v.shape[:-1] + (-1, 32))
    amax = np.abs(blocks).max(-1, keepdims=True)
    byte = np.maximum(np.where(amax > 0, np.frexp(amax)[1] - 1 + 127, 0) - down, 1)
    scale = np.exp2(byte - 127.0)
    codes = (blocks / scale).astype(np.float32).astype(dtype).astype(np.float64)
    return np.moveaxis((codes * scale).reshape(v.shape), -1, axis)


WIDE = False


def mx_kscale(k):
    if not WIDE:
        return np.ones(k)
    levels = np.array([10, -10, 5, -5, 0])
    a = np.random.permutation(np.resize(levels, k // 512 * 4)).reshape(k // 512, 4)
    idx = np.arange(k)
    return np.exp2(a[idx // 512, idx % 128 // 32])


BF16 = ml_dtypes.bfloat16


def bf(x):
    return np.asarray(x, np.float32).astype(BF16)


def f64(x):
    return np.asarray(x).astype(np.float64)


B, N, C, DIM, H = 4, 1024, 512, 1024, 8
D = DIM // H // 2
LAYER_NUM = 12
LAM_INIT = 0.8 - 0.6 * np.exp(-0.3 * LAYER_NUM)
SCALE = D ** -0.5


def split_qk(y):
    y = y.reshape(B, N, H, D, 2)
    return np.moveaxis(y, -1, 2).reshape(B, N, 2 * H, D)


def setup_inputs():
    s = mx_kscale(C)
    ls = 0.45 / D ** 0.25
    return {"x": bf(np.random.standard_normal((B, N, C)) * s),
            "Wq": bf(np.random.standard_normal((DIM, C)) / np.sqrt(C) / s),
            "Wk": bf(np.random.standard_normal((DIM, C)) / np.sqrt(C) / s),
            "lq1": bf(np.random.standard_normal(D) * ls),
            "lq2": bf(np.random.standard_normal(D) * ls),
            "lk1": bf(np.random.standard_normal(D) * ls),
            "lk2": bf(np.random.standard_normal(D) * ls)}


def reference(x, Wq, Wk, lq1, lq2, lk1, lk2):
    xq = mxq(f64(x), 2, "e4m3")
    q = split_qk(xq @ mxq(f64(Wq), 1, "e4m3").T) * SCALE
    k = split_qk(xq @ mxq(f64(Wk), 1, "e4m3").T)
    sc = np.stack([(q[:, :, i:i + 1, :] * k).sum(-1) for i in range(2 * H)], axis=2)
    e = np.exp(sc - sc.max(-1, keepdims=True))
    att = e / e.sum(-1, keepdims=True)
    lam = np.exp(np.sum(f64(lq1) * f64(lk1))) - np.exp(np.sum(f64(lq2) * f64(lk2))) + LAM_INIT
    return att[:, :, :H, :H] - lam * att[:, :, H:, H:]

@@ -1,0 +1,211 @@
+import math
+
+import concourse.mybir as mybir
+from concourse.masks import make_identity
+
+F32 = mybir.dt.float32
+BF16 = mybir.dt.bfloat16
+U32 = mybir.dt.uint32
+U8 = mybir.dt.uint8
+FP8X4 = mybir.dt.float8_e4m3fn_x4
+ALU = mybir.AluOpType
+ACT = mybir.ActivationFunctionType
+AXIS_X = mybir.AxisListType.X
+
+P = 128
+TOKENS = 4 * 1024
+C = 512
+WORDS = C // 2
+DIM = 1024
+ROWS = 16
+D = 64
+HEADS = 8
+BANK = 512
+TILES = TOKENS // P
+GROUP_TILES = 8
+SCALE = D ** -0.5
+LAM_INIT = 0.8 - 0.6 * math.exp(-0.3 * 12)
+
+CHUNK_ROWS = 2
+GPSIMD_ROWS = 10
+VECTOR_ROWS = ROWS - GPSIMD_ROWS
+
+FLOPS = 2 * TOKENS * C * 2 * DIM + 2 * TOKENS * ROWS * ROWS * D
+
+
+def transpose_words(nc, psum, ident, rows_f32, blocks):
+    planes = psum.tile([P, 2, blocks * P], F32, tag="planes")
+    for b in range(blocks):
+        for u in range(2):
+            nc.tensor.transpose(
+                planes[:, u, b * P : (b + 1) * P],
+                rows_f32[:, b * WORDS + u * P : b * WORDS + (u + 1) * P],
+                ident[:],
+            )
+    return planes
+
+
+def tile_differentialattention_pa_t_kernel(tc, x, Wq, Wk, lq1, lq2, lk1, lk2, out):
+    nc = tc.nc
+    x_rows = x.flatten_outer_dims()
+    out_rows = out.rearrange("b n a h -> (b n) (a h)")
+
+    with (
+        tc.tile_pool(name="keep", bufs=1) as keep,
+        tc.tile_pool(name="stage", bufs=2) as stage,
+        tc.tile_pool(name="work", bufs=2) as work,
+        tc.tile_pool(name="products", bufs=6) as products,
+        tc.psum_pool(name="psum_t", bufs=2) as psum_t,
+        tc.psum_pool(name="psum_y", bufs=2) as psum_y,
+    ):
+        ident = keep.tile([P, P], F32)
+        make_identity(nc, ident[:])
+
+        vectors = keep.tile([P, 4, D], BF16)
+        for v, vec in enumerate((lq1, lq2, lk1, lk2)):
+            nc.scalar.dma_start(out=vectors[:, v, :], in_=vec.partition_broadcast(P))
+        lam_products = keep.tile([P, 2, D], F32)
+        nc.vector.tensor_tensor(
+            out=lam_products[:], in0=vectors[:, 0:2, :], in1=vectors[:, 2:4, :], op=ALU.mult
+        )
+        lam_dots = keep.tile([P, 2], F32)
+        nc.vector.tensor_reduce(out=lam_dots[:], in_=lam_products[:], axis=AXIS_X, op=ALU.add)
+        lam_exps = keep.tile([P, 2], F32)
+        nc.scalar.activation(out=lam_exps[:], in_=lam_dots[:], func=ACT.Exp)
+        neg_lam = keep.tile([P, 1], F32)
+        nc.vector.tensor_tensor(
+            out=neg_lam[:], in0=lam_exps[:, 1:2], in1=lam_exps[:, 0:1], op=ALU.subtract
+        )
+        nc.vector.tensor_scalar_add(out=neg_lam[:], in0=neg_lam[:], scalar1=-LAM_INIT)
+
+        w_codes = []
+        w_scales = []
+        for name, W in (("q", Wq), ("k", Wk)):
+            w_sb = stage.tile([P, HEADS * C], BF16, tag="loaded")
+            nc.sync.dma_start(
+                out=w_sb[:].rearrange("p (h c) -> p h c", c=C),
+                in_=W.rearrange("(h p) c -> p h c", p=P),
+            )
+            w_f32 = w_sb[:].bitcast(F32)
+            grouped = stage.tile([P, DIM * 4], BF16, tag="grouped", align_bytes=64)
+            grouped_words = grouped[:].bitcast(F32).rearrange(
+                "p (j h d u) -> p j h d u", j=2, h=HEADS, d=D
+            )
+            for h0 in range(0, HEADS, 2):
+                planes = transpose_words(
+                    nc, psum_t, ident, w_f32[:, h0 * WORDS : (h0 + 2) * WORDS], 2
+                )
+                by_j = planes[:].rearrange("p u (hh d j) -> p j hh d u", hh=2, j=2)
+                for j in range(2):
+                    nc.scalar.copy(out=grouped_words[:, j, h0 : h0 + 2], in_=by_j[:, j])
+            codes = keep.tile([P, DIM], U32, name="codes_" + name, align_bytes=64)
+            scales = keep.tile([P, DIM], U8, name="scales_" + name, align_bytes=64)
+            nc.vector.quantize_mx(out=codes[:].bitcast(FP8X4), scales=scales[:], in_=grouped[:])
+            w_codes.append(codes)
+            w_scales.append(scales)
+
+        x_codes = keep.tile([P, TOKENS], U32, align_bytes=64)
+        x_scales = keep.tile([P, TOKENS], U8, align_bytes=64)
+        group_tokens = GROUP_TILES * P
+        for g in range(TILES // GROUP_TILES):
+            x_sb = stage.tile([P, GROUP_TILES * C], BF16, tag="loaded")
+            nc.sync.dma_start(
+                out=x_sb[:].rearrange("p (y c) -> p y c", c=C),
+                in_=x_rows[g * group_tokens : (g + 1) * group_tokens, :].rearrange(
+                    "(y p) c -> p y c", p=P
+                ),
+            )
+            x_f32 = x_sb[:].bitcast(F32)
+            grouped = stage.tile([P, group_tokens * 4], BF16, tag="grouped", align_bytes=64)
+            grouped_words = grouped[:].bitcast(F32).rearrange("p (w u) -> p w u", u=2)
+            for y0 in range(0, GROUP_TILES, 2):
+                planes = transpose_words(
+                    nc, psum_t, ident, x_f32[:, y0 * WORDS : (y0 + 2) * WORDS], 2
+                )
+                nc.scalar.copy(
+                    out=grouped_words[:, y0 * P : (y0 + 2) * P, :],
+                    in_=planes[:].rearrange("p u w -> p w u"),
+                )
+            cols = slice(g * group_tokens, (g + 1) * group_tokens)
+            nc.vector.quantize_mx(
+                out=x_codes[:, cols].bitcast(FP8X4), scales=x_scales[:, cols], in_=grouped[:]
+            )
+
+        for t in range(TILES):
+            tok = slice(t * P, (t + 1) * P)
+
+            def project(w, half, tag):
+                y = psum_y.tile([P, BANK], F32, tag=tag)
+                cols = slice(half * BANK, (half + 1) * BANK)
+                nc.tensor.matmul_mx(
+                    out=y[:],
+                    lhsT=x_codes[:, tok].bitcast(FP8X4),
+                    lhsT_scale=x_scales[:, tok],
+                    rhs=w_codes[w][:, cols].bitcast(FP8X4),
+                    rhs_scale=w_scales[w][:, cols],
+                    start=True,
+                    stop=True,
+                )
+                return y
+
+            k_sb = work.tile([P, DIM], F32)
+            q_sb = work.tile([P, DIM], F32)
+            q_low = project(0, 0, "q_low")
+            nc.scalar.copy(out=q_sb[:, VECTOR_ROWS * D : BANK], in_=q_low[:, VECTOR_ROWS * D :])
+            q_high = project(0, 1, "to_sbuf")
+            nc.scalar.copy(out=q_sb[:, BANK:], in_=q_high[:])
+            for half in range(2):
+                k_half = project(1, half, "to_sbuf")
+                nc.scalar.copy(out=k_sb[:, half * BANK : (half + 1) * BANK], in_=k_half[:])
+
+            chunk_shape = [P, CHUNK_ROWS, ROWS, D]
+            k_all = k_sb[:].rearrange("p (m d) -> p m d", d=D).unsqueeze(1).to_broadcast(chunk_shape)
+            scores = work.tile([P, ROWS, ROWS], F32)
+            for i0 in range(0, ROWS, CHUNK_ROWS):
+                q_cols = slice(i0 * D, (i0 + CHUNK_ROWS) * D)
+                prod = products.tile(chunk_shape, F32)
+                if i0 < VECTOR_ROWS:
+                    q_chunk = q_low[:, q_cols]
+                    engine = nc.vector
+                else:
+                    q_chunk = q_sb[:, q_cols]
+                    engine = nc.gpsimd
+                engine.tensor_tensor(
+                    out=prod[:],
+                    in0=q_chunk.rearrange("p (i d) -> p i d", d=D).unsqueeze(2).to_broadcast(chunk_shape),
+                    in1=k_all,
+                    op=ALU.mult,
+                )
+                nc.vector.tensor_reduce(
+                    out=scores[:, i0 : i0 + CHUNK_ROWS, :], in_=prod[:], axis=AXIS_X, op=ALU.add
+                )
+
+            row_shape = [P, ROWS, ROWS]
+            row_max = work.tile([P, ROWS], F32)
+            nc.vector.tensor_reduce(out=row_max[:], in_=scores[:], axis=AXIS_X, op=ALU.max)
+            nc.vector.tensor_tensor(
+                out=scores[:],
+                in0=scores[:],
+                in1=row_max[:].unsqueeze(2).to_broadcast(row_shape),
+                op=ALU.subtract,
+            )
+            exps = work.tile(row_shape, F32)
+            nc.scalar.activation(out=exps[:], in_=scores[:], func=ACT.Exp, scale=SCALE)
+            row_sum = work.tile([P, ROWS], F32)
+            nc.vector.tensor_reduce(out=row_sum[:], in_=exps[:], axis=AXIS_X, op=ALU.add)
+            factor = work.tile([P, ROWS], F32)
+            nc.vector.reciprocal(out=factor[:], in_=row_sum[:])
+            nc.vector.tensor_scalar_mul(
+                out=factor[:, HEADS:], in0=factor[:, HEADS:], scalar1=neg_lam[:, 0:1]
+            )
+            nc.vector.tensor_tensor(
+                out=exps[:],
+                in0=exps[:],
+                in1=factor[:].unsqueeze(2).to_broadcast(row_shape),
+                op=ALU.mult,
+            )
+            result = work.tile([P, HEADS, HEADS], F32)
+            nc.vector.tensor_tensor(
+                out=result[:], in0=exps[:, :HEADS, :HEADS], in1=exps[:, HEADS:, HEADS:], op=ALU.add
+            )
+            nc.sync.dma_start(out=out_rows[tok, :], in_=result[:].rearrange("p a h -> p (a h)"))

@@ -5,6 +5,7 @@ from concourse.masks import make_identity
 
 F32 = mybir.dt.float32
 BF16 = mybir.dt.bfloat16
+I32 = mybir.dt.int32
 U32 = mybir.dt.uint32
 U8 = mybir.dt.uint8
 FP8X4 = mybir.dt.float8_e4m3fn_x4
@@ -13,24 +14,38 @@ ACT = mybir.ActivationFunctionType
 AXIS_X = mybir.AxisListType.X
 
 P = 128
+HALF = P // 2
+QUADRANT = 32
 TOKENS = 4 * 1024
 C = 512
 WORDS = C // 2
-DIM = 1024
 ROWS = 16
 D = 64
 HEADS = 8
 BANK = 512
-TILES = TOKENS // P
-GROUP_TILES = 8
+BANK_ROWS = 4
 SCALE = D ** -0.5
 LAM_INIT = 0.8 - 0.6 * math.exp(-0.3 * 12)
 
-CHUNK_ROWS = 2
-GPSIMD_ROWS = 10
-VECTOR_ROWS = ROWS - GPSIMD_ROWS
+GROUP_TILES = 8
+GROUP_TOKENS = GROUP_TILES * P
+GROUPS = TOKENS // GROUP_TOKENS
+TENSOR_GROUPS = 3
+TILE_PAIRS = GROUP_TILES // 2
+BLOCKS = 4
+BLOCK_T = P // BLOCKS
+BLOCK_TOKENS = GROUP_TILES * BLOCK_T
+SCORE_COLS = ROWS * TILE_PAIRS
+BANK_MATMULS = BANK // SCORE_COLS
 
-FLOPS = 2 * TOKENS * C * 2 * DIM + 2 * TOKENS * ROWS * ROWS * D
+PADDED = 2 * ROWS * D
+PADDED_ALL = PADDED + D
+
+CHUNK_ROWS = 2
+VECTOR_ROWS = BANK_ROWS
+BATCH_TILES = 4
+
+FLOPS = 2 * TOKENS * C * 2 * ROWS * D + 2 * TOKENS * ROWS * ROWS * D
 
 
 def transpose_words(nc, psum, ident, rows_f32, blocks):
@@ -53,13 +68,22 @@ def tile_differentialattention_pa_t_kernel(tc, x, Wq, Wk, lq1, lq2, lk1, lk2, ou
     with (
         tc.tile_pool(name="keep", bufs=1) as keep,
         tc.tile_pool(name="stage", bufs=2) as stage,
-        tc.tile_pool(name="work", bufs=2) as work,
-        tc.tile_pool(name="products", bufs=6) as products,
+        tc.tile_pool(name="tensor_way", bufs=1) as tensor_way,
+        tc.tile_pool(name="vector_way", bufs=2) as vector_way,
+        tc.tile_pool(name="products", bufs=4) as products,
         tc.psum_pool(name="psum_t", bufs=2) as psum_t,
-        tc.psum_pool(name="psum_y", bufs=2) as psum_y,
+        tc.psum_pool(name="psum_y", bufs=3) as psum_y,
+        tc.psum_pool(name="psum_s", bufs=2) as psum_s,
+        tc.psum_pool(name="psum_q", bufs=1) as psum_q,
     ):
         ident = keep.tile([P, P], F32)
         make_identity(nc, ident[:])
+
+        q_diag = []
+        for turn in range(2):
+            diag = keep.tile([P, BLOCK_T, TILE_PAIRS, 2, ROWS], F32, name="q_diag%d" % turn)
+            nc.gpsimd.memset(diag[:], 0.0)
+            q_diag.append(diag)
 
         vectors = keep.tile([P, 4, D], BF16)
         for v, vec in enumerate((lq1, lq2, lk1, lk2)):
@@ -77,135 +101,292 @@ def tile_differentialattention_pa_t_kernel(tc, x, Wq, Wk, lq1, lq2, lk1, lk2, ou
             out=neg_lam[:], in0=lam_exps[:, 1:2], in1=lam_exps[:, 0:1], op=ALU.subtract
         )
         nc.vector.tensor_scalar_add(out=neg_lam[:], in0=neg_lam[:], scalar1=-LAM_INIT)
+        parity = keep.tile([P, 2], F32)
+        nc.vector.tensor_reduce(
+            out=parity[:],
+            in_=ident[:].rearrange("p (c j) -> p j c", j=2),
+            axis=AXIS_X,
+            op=ALU.add,
+        )
+        odd_neg_lam = keep.tile([P, 1], F32)
+        nc.vector.tensor_tensor(out=odd_neg_lam[:], in0=parity[:, 1:2], in1=neg_lam[:], op=ALU.mult)
 
         w_codes = []
         w_scales = []
         for name, W in (("q", Wq), ("k", Wk)):
-            w_sb = stage.tile([P, HEADS * C], BF16, tag="loaded")
+            w_sb = stage.tile([P, HEADS * C], BF16, tag="loaded", bufs=3)
             nc.sync.dma_start(
-                out=w_sb[:].rearrange("p (h c) -> p h c", c=C),
-                in_=W.rearrange("(h p) c -> p h c", p=P),
+                out=w_sb[:].rearrange("p (a c) -> p a c", c=C),
+                in_=W.rearrange("(a p) c -> p a c", p=P),
             )
             w_f32 = w_sb[:].bitcast(F32)
-            grouped = stage.tile([P, DIM * 4], BF16, tag="grouped", align_bytes=64)
-            grouped_words = grouped[:].bitcast(F32).rearrange(
-                "p (j h d u) -> p j h d u", j=2, h=HEADS, d=D
-            )
-            for h0 in range(0, HEADS, 2):
-                planes = transpose_words(
-                    nc, psum_t, ident, w_f32[:, h0 * WORDS : (h0 + 2) * WORDS], 2
+            codes = keep.tile([P, PADDED_ALL], U32, name="codes_" + name, align_bytes=64)
+            scales = keep.tile([P, PADDED_ALL], U8, name="scales_" + name, align_bytes=64)
+            nc.vector.memset(codes[:, PADDED:].bitcast(I32), 0)
+            nc.vector.memset(scales[:, PADDED:].bitcast(I32), 0)
+            for part in range(2):
+                grouped = stage.tile([P, 4 * PADDED // 2], BF16, tag="grouped", align_bytes=64)
+                grouped_words = grouped[:].bitcast(F32)
+                nc.vector.memset(grouped_words, 0.0)
+                by_row = grouped_words.rearrange(
+                    "p (a j z d u) -> p a j z d u", a=HEADS // 2, j=2, z=2, d=D
                 )
-                by_j = planes[:].rearrange("p u (hh d j) -> p j hh d u", hh=2, j=2)
-                for j in range(2):
-                    nc.scalar.copy(out=grouped_words[:, j, h0 : h0 + 2], in_=by_j[:, j])
-            codes = keep.tile([P, DIM], U32, name="codes_" + name, align_bytes=64)
-            scales = keep.tile([P, DIM], U8, name="scales_" + name, align_bytes=64)
-            nc.vector.quantize_mx(out=codes[:].bitcast(FP8X4), scales=scales[:], in_=grouped[:])
+                for a0 in range(0, HEADS // 2, 2):
+                    first = (part * (HEADS // 2) + a0) * WORDS
+                    planes = transpose_words(nc, psum_t, ident, w_f32[:, first : first + 2 * WORDS], 2)
+                    by_j = planes[:].rearrange("p u (a d j) -> p j a d u", a=2, j=2)
+                    for j in range(2):
+                        nc.scalar.copy(out=by_row[:, a0 : a0 + 2, j, 1], in_=by_j[:, j])
+                cols = slice(part * PADDED // 2, (part + 1) * PADDED // 2)
+                nc.vector.quantize_mx(
+                    out=codes[:, cols].bitcast(FP8X4), scales=scales[:, cols], in_=grouped[:]
+                )
             w_codes.append(codes)
             w_scales.append(scales)
 
         x_codes = keep.tile([P, TOKENS], U32, align_bytes=64)
         x_scales = keep.tile([P, TOKENS], U8, align_bytes=64)
-        group_tokens = GROUP_TILES * P
-        for g in range(TILES // GROUP_TILES):
-            x_sb = stage.tile([P, GROUP_TILES * C], BF16, tag="loaded")
+        for g in [GROUPS - 1] + list(range(TENSOR_GROUPS)):
+            x_sb = stage.tile([P, GROUP_TILES * C], BF16, tag="loaded", bufs=3)
             nc.sync.dma_start(
                 out=x_sb[:].rearrange("p (y c) -> p y c", c=C),
-                in_=x_rows[g * group_tokens : (g + 1) * group_tokens, :].rearrange(
+                in_=x_rows[g * GROUP_TOKENS : (g + 1) * GROUP_TOKENS, :].rearrange(
                     "(y p) c -> p y c", p=P
                 ),
             )
             x_f32 = x_sb[:].bitcast(F32)
-            grouped = stage.tile([P, group_tokens * 4], BF16, tag="grouped", align_bytes=64)
-            grouped_words = grouped[:].bitcast(F32).rearrange("p (w u) -> p w u", u=2)
-            for y0 in range(0, GROUP_TILES, 2):
+            grouped = stage.tile([P, 4 * GROUP_TOKENS], BF16, tag="grouped", align_bytes=64)
+            in_order = grouped[:].bitcast(F32).rearrange("p (w u) -> p w u", u=2)
+            by_block = grouped[:].bitcast(F32).rearrange(
+                "p (b s n t u) -> p b s n t u", b=BLOCKS, s=2, n=TILE_PAIRS, u=2
+            )
+            for n in range(TILE_PAIRS):
                 planes = transpose_words(
-                    nc, psum_t, ident, x_f32[:, y0 * WORDS : (y0 + 2) * WORDS], 2
+                    nc, psum_t, ident, x_f32[:, 2 * n * WORDS : (2 * n + 2) * WORDS], 2
                 )
-                nc.scalar.copy(
-                    out=grouped_words[:, y0 * P : (y0 + 2) * P, :],
-                    in_=planes[:].rearrange("p u w -> p w u"),
-                )
-            cols = slice(g * group_tokens, (g + 1) * group_tokens)
+                if g < TENSOR_GROUPS:
+                    for s in range(2):
+                        nc.scalar.copy(
+                            out=by_block[:, :, s, n],
+                            in_=planes[:, :, s * P : (s + 1) * P].rearrange(
+                                "p u (b t) -> p b t u", b=BLOCKS
+                            ),
+                        )
+                else:
+                    nc.scalar.copy(
+                        out=in_order[:, 2 * n * P : (2 * n + 2) * P, :],
+                        in_=planes[:].rearrange("p u w -> p w u"),
+                    )
+            cols = slice(g * GROUP_TOKENS, (g + 1) * GROUP_TOKENS)
             nc.vector.quantize_mx(
                 out=x_codes[:, cols].bitcast(FP8X4), scales=x_scales[:, cols], in_=grouped[:]
             )
 
-        for t in range(TILES):
-            tok = slice(t * P, (t + 1) * P)
+        def project_pairs(w, bank_index, first_token):
+            bank = psum_y.tile([P, BANK_ROWS, P], F32, tag="y")
+            for i in range(BANK_ROWS):
+                r = bank_index * BANK_ROWS + i
+                for s in range(2):
+                    w_cols = slice(P * r + D * (1 - s), P * r + D * (1 - s) + P)
+                    x_cols = slice(first_token + s * P, first_token + (s + 1) * P)
+                    nc.tensor.matmul_mx(
+                        out=bank[:, i, :],
+                        lhsT=w_codes[w][:, w_cols].bitcast(FP8X4),
+                        lhsT_scale=w_scales[w][:, w_cols],
+                        rhs=x_codes[:, x_cols].bitcast(FP8X4),
+                        rhs_scale=x_scales[:, x_cols],
+                        start=(s == 0),
+                        stop=(s == 1),
+                    )
+            return bank
 
-            def project(w, half, tag):
-                y = psum_y.tile([P, BANK], F32, tag=tag)
-                cols = slice(half * BANK, (half + 1) * BANK)
-                nc.tensor.matmul_mx(
-                    out=y[:],
-                    lhsT=x_codes[:, tok].bitcast(FP8X4),
-                    lhsT_scale=x_scales[:, tok],
-                    rhs=w_codes[w][:, cols].bitcast(FP8X4),
-                    rhs_scale=w_scales[w][:, cols],
-                    start=True,
-                    stop=True,
+        def score_block(g, b, diag, dense):
+            first_token = g * GROUP_TOKENS + b * BLOCK_TOKENS
+            for bank_index in range(ROWS // BANK_ROWS):
+                rows = slice(bank_index * BANK_ROWS, (bank_index + 1) * BANK_ROWS)
+                bank = project_pairs(0, bank_index, first_token)
+                for s in range(2):
+                    half = slice(s * HALF, (s + 1) * HALF)
+                    nc.scalar.copy(
+                        out=diag[half, :, :, s, rows],
+                        in_=bank[half].rearrange("p i (n t) -> p t n i", n=TILE_PAIRS),
+                    )
+            k_pairs = tensor_way.tile([P, BLOCK_T, ROWS, TILE_PAIRS], F32, bufs=2)
+            for bank_index in range(ROWS // BANK_ROWS):
+                rows = slice(bank_index * BANK_ROWS, (bank_index + 1) * BANK_ROWS)
+                bank = project_pairs(1, bank_index, first_token)
+                nc.scalar.copy(
+                    out=k_pairs[:, :, rows, :],
+                    in_=bank[:].rearrange("p i (n t) -> p t i n", n=TILE_PAIRS),
                 )
-                return y
+            for t0 in range(0, BLOCK_T, BANK_MATMULS):
+                raw = psum_s.tile([P, BANK_MATMULS, SCORE_COLS], F32, tag="raw")
+                for i in range(BANK_MATMULS):
+                    nc.tensor.matmul(
+                        out=raw[:, i, :],
+                        lhsT=diag[:, t0 + i].rearrange("p n s r -> p (n s r)"),
+                        rhs=k_pairs[:, t0 + i].rearrange("p m n -> p (m n)"),
+                        start=True,
+                        stop=True,
+                    )
+                for n in range(TILE_PAIRS):
+                    quad = slice(n * QUADRANT, (n + 1) * QUADRANT)
+                    first = b * BLOCK_T + t0
+                    nc.scalar.copy(
+                        out=dense[quad, first : first + BANK_MATMULS, :],
+                        in_=raw[quad].rearrange("p i (m n) -> p i m n", n=TILE_PAIRS)[:, :, :, n],
+                    )
 
-            k_sb = work.tile([P, DIM], F32)
-            q_sb = work.tile([P, DIM], F32)
-            q_low = project(0, 0, "q_low")
-            nc.scalar.copy(out=q_sb[:, VECTOR_ROWS * D : BANK], in_=q_low[:, VECTOR_ROWS * D :])
-            q_high = project(0, 1, "to_sbuf")
-            nc.scalar.copy(out=q_sb[:, BANK:], in_=q_high[:])
-            for half in range(2):
-                k_half = project(1, half, "to_sbuf")
-                nc.scalar.copy(out=k_sb[:, half * BANK : (half + 1) * BANK], in_=k_half[:])
+        def finish_group(g, dense):
+            dense_shape = [P, P, ROWS]
+            row_max = tensor_way.tile([P, P], F32)
+            nc.vector.tensor_reduce(out=row_max[:], in_=dense[:], axis=AXIS_X, op=ALU.max)
+            nc.vector.tensor_tensor(
+                out=dense[:],
+                in0=dense[:],
+                in1=row_max[:].unsqueeze(2).to_broadcast(dense_shape),
+                op=ALU.subtract,
+            )
+            nc.scalar.activation(out=dense[:], in_=dense[:], func=ACT.Exp, scale=SCALE)
+            row_sum = tensor_way.tile([P, P], F32)
+            nc.vector.tensor_reduce(out=row_sum[:], in_=dense[:], axis=AXIS_X, op=ALU.add)
+            inverse = tensor_way.tile([P, P], F32)
+            nc.vector.reciprocal(out=inverse[:], in_=row_sum[:])
+            by_parity = dense[:].rearrange("p t (h j) -> p j h t", j=2)
+            odd_part = tensor_way.tile([P, HEADS, P], F32)
+            nc.scalar.activation(
+                out=odd_part[:], in_=by_parity[:, 1], func=ACT.Copy, scale=odd_neg_lam[:, 0:1]
+            )
+            picked = tensor_way.tile([P, HEADS, P], F32)
+            nc.vector.scalar_tensor_tensor(
+                out=picked[:],
+                in0=by_parity[:, 0],
+                scalar=parity[:, 0:1],
+                in1=odd_part[:],
+                op0=ALU.mult,
+                op1=ALU.add,
+            )
+            nc.vector.tensor_tensor(
+                out=picked[:],
+                in0=picked[:],
+                in1=inverse[:].unsqueeze(1).to_broadcast([P, HEADS, P]),
+                op=ALU.mult,
+            )
+            result = tensor_way.tile([P, GROUP_TILES, HEADS, HEADS], F32)
+            result_rows = result[:].rearrange("p y a h -> p (y a) h")
+            for h0 in range(0, HEADS, BANK_ROWS):
+                flipped = psum_t.tile([P, BANK_ROWS, P], F32, tag="planes")
+                for i in range(BANK_ROWS):
+                    nc.tensor.transpose(flipped[:, i, :], picked[:, h0 + i, :], ident[:])
+                nc.vector.tensor_reduce(
+                    out=result_rows[:, :, h0 : h0 + BANK_ROWS],
+                    in_=flipped[:].rearrange("p i (e j) -> p e i j", j=2),
+                    axis=AXIS_X,
+                    op=ALU.add,
+                )
+            nc.sync.dma_start(
+                out=out_rows[g * GROUP_TOKENS : (g + 1) * GROUP_TOKENS, :].rearrange(
+                    "(y p) e -> p y e", p=P
+                ),
+                in_=result[:].rearrange("p y a h -> p y (a h)"),
+            )
 
+        def project_tile(w, bank_index, tok, pool, tag):
+            bank = pool.tile([P, BANK], F32, tag=tag)
+            w_cols = slice(D + bank_index * BANK, D + (bank_index + 1) * BANK)
+            nc.tensor.matmul_mx(
+                out=bank[:],
+                lhsT=x_codes[:, tok].bitcast(FP8X4),
+                lhsT_scale=x_scales[:, tok],
+                rhs=w_codes[w][:, w_cols].bitcast(FP8X4),
+                rhs_scale=w_scales[w][:, w_cols],
+                start=True,
+                stop=True,
+            )
+            return bank[:].rearrange("p (i z d) -> p i z d", z=2, d=D)[:, :, 0, :]
+
+        def score_tile(tile_index, scores):
+            tok = slice(tile_index * P, (tile_index + 1) * P)
+            q_psum = project_tile(0, 0, tok, psum_q, "q")
+            q_sb = vector_way.tile([P, ROWS, D], F32)
+            k_sb = vector_way.tile([P, ROWS, D], F32)
+            for bank_index in range(ROWS // BANK_ROWS):
+                rows = slice(bank_index * BANK_ROWS, (bank_index + 1) * BANK_ROWS)
+                nc.scalar.copy(out=k_sb[:, rows, :], in_=project_tile(1, bank_index, tok, psum_y, "y"))
+                if bank_index > 0:
+                    nc.scalar.copy(
+                        out=q_sb[:, rows, :], in_=project_tile(0, bank_index, tok, psum_y, "y")
+                    )
             chunk_shape = [P, CHUNK_ROWS, ROWS, D]
-            k_all = k_sb[:].rearrange("p (m d) -> p m d", d=D).unsqueeze(1).to_broadcast(chunk_shape)
-            scores = work.tile([P, ROWS, ROWS], F32)
-            for i0 in range(0, ROWS, CHUNK_ROWS):
-                q_cols = slice(i0 * D, (i0 + CHUNK_ROWS) * D)
+            for r0 in range(0, ROWS, CHUNK_ROWS):
+                rows = slice(r0, r0 + CHUNK_ROWS)
                 prod = products.tile(chunk_shape, F32)
-                if i0 < VECTOR_ROWS:
-                    q_chunk = q_low[:, q_cols]
+                if r0 < VECTOR_ROWS:
+                    q_chunk = q_psum[:, rows, :]
                     engine = nc.vector
                 else:
-                    q_chunk = q_sb[:, q_cols]
+                    q_chunk = q_sb[:, rows, :]
                     engine = nc.gpsimd
                 engine.tensor_tensor(
                     out=prod[:],
-                    in0=q_chunk.rearrange("p (i d) -> p i d", d=D).unsqueeze(2).to_broadcast(chunk_shape),
-                    in1=k_all,
+                    in0=q_chunk.unsqueeze(2).to_broadcast(chunk_shape),
+                    in1=k_sb[:].unsqueeze(1).to_broadcast(chunk_shape),
                     op=ALU.mult,
                 )
-                nc.vector.tensor_reduce(
-                    out=scores[:, i0 : i0 + CHUNK_ROWS, :], in_=prod[:], axis=AXIS_X, op=ALU.add
-                )
+                nc.vector.tensor_reduce(out=scores[:, rows, :], in_=prod[:], axis=AXIS_X, op=ALU.add)
 
-            row_shape = [P, ROWS, ROWS]
-            row_max = work.tile([P, ROWS], F32)
-            nc.vector.tensor_reduce(out=row_max[:], in_=scores[:], axis=AXIS_X, op=ALU.max)
+        def finish_batch(first_tile, batch):
+            batch_rows = BATCH_TILES * ROWS
+            batch_shape = [P, batch_rows, ROWS]
+            row_max = vector_way.tile([P, batch_rows], F32)
+            nc.vector.tensor_reduce(out=row_max[:], in_=batch[:], axis=AXIS_X, op=ALU.max)
             nc.vector.tensor_tensor(
-                out=scores[:],
-                in0=scores[:],
-                in1=row_max[:].unsqueeze(2).to_broadcast(row_shape),
+                out=batch[:],
+                in0=batch[:],
+                in1=row_max[:].unsqueeze(2).to_broadcast(batch_shape),
                 op=ALU.subtract,
             )
-            exps = work.tile(row_shape, F32)
-            nc.scalar.activation(out=exps[:], in_=scores[:], func=ACT.Exp, scale=SCALE)
-            row_sum = work.tile([P, ROWS], F32)
-            nc.vector.tensor_reduce(out=row_sum[:], in_=exps[:], axis=AXIS_X, op=ALU.add)
-            factor = work.tile([P, ROWS], F32)
+            nc.scalar.activation(out=batch[:], in_=batch[:], func=ACT.Exp, scale=SCALE)
+            row_sum = vector_way.tile([P, batch_rows], F32)
+            nc.vector.tensor_reduce(out=row_sum[:], in_=batch[:], axis=AXIS_X, op=ALU.add)
+            factor = vector_way.tile([P, batch_rows], F32)
             nc.vector.reciprocal(out=factor[:], in_=row_sum[:])
-            nc.vector.tensor_scalar_mul(
-                out=factor[:, HEADS:], in0=factor[:, HEADS:], scalar1=neg_lam[:, 0:1]
-            )
+            odd_rows = factor[:].rearrange("p (e j) -> p e j", j=2)[:, :, 1]
+            nc.vector.tensor_scalar_mul(out=odd_rows, in0=odd_rows, scalar1=neg_lam[:, 0:1])
             nc.vector.tensor_tensor(
-                out=exps[:],
-                in0=exps[:],
-                in1=factor[:].unsqueeze(2).to_broadcast(row_shape),
+                out=batch[:],
+                in0=batch[:],
+                in1=factor[:].unsqueeze(2).to_broadcast(batch_shape),
                 op=ALU.mult,
             )
-            result = work.tile([P, HEADS, HEADS], F32)
+            by_parity = batch[:].rearrange("p (e j) (h i) -> p e j h i", j=2, i=2)
+            result = vector_way.tile([P, BATCH_TILES * HEADS, HEADS], F32)
             nc.vector.tensor_tensor(
-                out=result[:], in0=exps[:, :HEADS, :HEADS], in1=exps[:, HEADS:, HEADS:], op=ALU.add
+                out=result[:], in0=by_parity[:, :, 0, :, 0], in1=by_parity[:, :, 1, :, 1], op=ALU.add
             )
-            nc.sync.dma_start(out=out_rows[tok, :], in_=result[:].rearrange("p a h -> p (a h)"))
+            nc.sync.dma_start(
+                out=out_rows[first_tile * P : (first_tile + BATCH_TILES) * P, :].rearrange(
+                    "(y p) e -> p y e", p=P
+                ),
+                in_=result[:].rearrange("p (y a) h -> p y (a h)", a=HEADS),
+            )
+
+        vector_tile = 0
+        for step in range(TENSOR_GROUPS * BLOCKS):
+            g = step // BLOCKS
+            b = step % BLOCKS
+            if step % 3 < 2:
+                if vector_tile % BATCH_TILES == 0:
+                    batch = vector_way.tile([P, BATCH_TILES * ROWS, ROWS], F32)
+                i = vector_tile % BATCH_TILES
+                score_tile(
+                    TENSOR_GROUPS * GROUP_TILES + vector_tile, batch[:, i * ROWS : (i + 1) * ROWS, :]
+                )
+                vector_tile += 1
+                if vector_tile % BATCH_TILES == 0:
+                    finish_batch(TENSOR_GROUPS * GROUP_TILES + vector_tile - BATCH_TILES, batch)
+            if b == 0:
+                dense = tensor_way.tile([P, P, ROWS], F32, bufs=2)
+            score_block(g, b, q_diag[step % 2], dense)
+            if b == BLOCKS - 1:
+                finish_group(g, dense)

@@ -41,9 +41,10 @@ BANK_MATMULS = BANK // SCORE_COLS
 PADDED = 2 * ROWS * D
 PADDED_ALL = PADDED + D
 
-CHUNK_ROWS = 2
-VECTOR_ROWS = BANK_ROWS
-BATCH_TILES = 4
+VECTOR_ROWS = 7
+VECTOR_BANKS = 2
+SCALAR_SUM_ROWS = 4
+BATCH_TILES = 2
 
 FLOPS = 2 * TOKENS * C * 2 * ROWS * D + 2 * TOKENS * ROWS * ROWS * D
 
@@ -70,9 +71,9 @@ def tile_differentialattention_pa_t_kernel(tc, x, Wq, Wk, lq1, lq2, lk1, lk2, ou
         tc.tile_pool(name="stage", bufs=2) as stage,
         tc.tile_pool(name="tensor_way", bufs=1) as tensor_way,
         tc.tile_pool(name="vector_way", bufs=2) as vector_way,
-        tc.tile_pool(name="products", bufs=4) as products,
+        tc.tile_pool(name="products", bufs=8) as products,
         tc.psum_pool(name="psum_t", bufs=2) as psum_t,
-        tc.psum_pool(name="psum_y", bufs=3) as psum_y,
+        tc.psum_pool(name="psum_y", bufs=2) as psum_y,
         tc.psum_pool(name="psum_s", bufs=2) as psum_s,
         tc.psum_pool(name="psum_q", bufs=1) as psum_q,
     ):
@@ -135,8 +136,9 @@ def tile_differentialattention_pa_t_kernel(tc, x, Wq, Wk, lq1, lq2, lk1, lk2, ou
                     first = (part * (HEADS // 2) + a0) * WORDS
                     planes = transpose_words(nc, psum_t, ident, w_f32[:, first : first + 2 * WORDS], 2)
                     by_j = planes[:].rearrange("p u (a d j) -> p j a d u", a=2, j=2)
+                    copy = nc.scalar.copy if a0 == 0 else nc.vector.tensor_copy
                     for j in range(2):
-                        nc.scalar.copy(out=by_row[:, a0 : a0 + 2, j, 1], in_=by_j[:, j])
+                        copy(out=by_row[:, a0 : a0 + 2, j, 1], in_=by_j[:, j])
                 cols = slice(part * PADDED // 2, (part + 1) * PADDED // 2)
                 nc.vector.quantize_mx(
                     out=codes[:, cols].bitcast(FP8X4), scales=scales[:, cols], in_=grouped[:]
@@ -173,7 +175,8 @@ def tile_differentialattention_pa_t_kernel(tc, x, Wq, Wk, lq1, lq2, lk1, lk2, ou
                             ),
                         )
                 else:
-                    nc.scalar.copy(
+                    copy = nc.scalar.copy if n % 2 == 0 else nc.vector.tensor_copy
+                    copy(
                         out=in_order[:, 2 * n * P : (2 * n + 2) * P, :],
                         in_=planes[:].rearrange("p u w -> p w u"),
                     )
@@ -307,33 +310,49 @@ def tile_differentialattention_pa_t_kernel(tc, x, Wq, Wk, lq1, lq2, lk1, lk2, ou
 
         def score_tile(tile_index, scores):
             tok = slice(tile_index * P, (tile_index + 1) * P)
-            q_psum = project_tile(0, 0, tok, psum_q, "q")
             q_sb = vector_way.tile([P, ROWS, D], F32)
             k_sb = vector_way.tile([P, ROWS, D], F32)
+            q_psum = []
             for bank_index in range(ROWS // BANK_ROWS):
-                rows = slice(bank_index * BANK_ROWS, (bank_index + 1) * BANK_ROWS)
-                nc.scalar.copy(out=k_sb[:, rows, :], in_=project_tile(1, bank_index, tok, psum_y, "y"))
-                if bank_index > 0:
+                first = bank_index * BANK_ROWS
+                nc.scalar.copy(
+                    out=k_sb[:, first : first + BANK_ROWS, :],
+                    in_=project_tile(1, bank_index, tok, psum_y, "y"),
+                )
+                if bank_index < VECTOR_BANKS:
+                    q_bank = project_tile(0, bank_index, tok, psum_q, "q%d" % bank_index)
+                    q_psum.append(q_bank)
+                else:
+                    q_bank = project_tile(0, bank_index, tok, psum_y, "y")
+                skip = min(max(VECTOR_ROWS - first, 0), BANK_ROWS)
+                if skip < BANK_ROWS:
                     nc.scalar.copy(
-                        out=q_sb[:, rows, :], in_=project_tile(0, bank_index, tok, psum_y, "y")
+                        out=q_sb[:, first + skip : first + BANK_ROWS, :], in_=q_bank[:, skip:, :]
                     )
-            chunk_shape = [P, CHUNK_ROWS, ROWS, D]
-            for r0 in range(0, ROWS, CHUNK_ROWS):
-                rows = slice(r0, r0 + CHUNK_ROWS)
-                prod = products.tile(chunk_shape, F32)
-                if r0 < VECTOR_ROWS:
-                    q_chunk = q_psum[:, rows, :]
+            row_shape = [P, ROWS, D]
+            for r in range(ROWS):
+                prod = products.tile(row_shape, F32)
+                if r < VECTOR_ROWS:
+                    q_row = q_psum[r // BANK_ROWS][:, r % BANK_ROWS : r % BANK_ROWS + 1, :]
                     engine = nc.vector
                 else:
-                    q_chunk = q_sb[:, rows, :]
+                    q_row = q_sb[:, r : r + 1, :]
                     engine = nc.gpsimd
                 engine.tensor_tensor(
-                    out=prod[:],
-                    in0=q_chunk.unsqueeze(2).to_broadcast(chunk_shape),
-                    in1=k_sb[:].unsqueeze(1).to_broadcast(chunk_shape),
-                    op=ALU.mult,
+                    out=prod[:], in0=q_row.to_broadcast(row_shape), in1=k_sb[:], op=ALU.mult
                 )
-                nc.vector.tensor_reduce(out=scores[:, rows, :], in_=prod[:], axis=AXIS_X, op=ALU.add)
+                if r < ROWS - SCALAR_SUM_ROWS:
+                    nc.vector.tensor_reduce(
+                        out=scores[:, r, :], in_=prod[:], axis=AXIS_X, op=ALU.add
+                    )
+                else:
+                    for m in range(ROWS):
+                        nc.scalar.activation(
+                            out=prod[:, m, :],
+                            in_=prod[:, m, :],
+                            func=ACT.Copy,
+                            accum_out=scores[:, r, m : m + 1],
+                        )
 
         def finish_batch(first_tile, batch):
             batch_rows = BATCH_TILES * ROWS

@@ -35,16 +35,25 @@ TILE_PAIRS = GROUP_TILES // 2
 BLOCKS = 4
 BLOCK_T = P // BLOCKS
 BLOCK_TOKENS = GROUP_TILES * BLOCK_T
+X_PIECES = TILE_PAIRS + 1
 SCORE_COLS = ROWS * TILE_PAIRS
 BANK_MATMULS = BANK // SCORE_COLS
 
 PADDED = 2 * ROWS * D
 PADDED_ALL = PADDED + D
 
-VECTOR_ROWS = 7
-VECTOR_BANKS = 2
-SCALAR_SUM_ROWS = 4
+VECTOR_TILES = GROUP_TILES
+ROW_PAIRS = ROWS // 2
+ALL_PAIRS = VECTOR_TILES * ROW_PAIRS
+VECTOR_BANKS = ROW_PAIRS // BANK_ROWS
+SCALAR_SUMS = 3
+LAG = 2
 BATCH_TILES = 2
+BATCH_PAIRS = BATCH_TILES * ROW_PAIRS
+
+BLOCK_STEPS = ROWS // BANK_ROWS
+GROUP_STEPS = BLOCKS * BLOCK_STEPS
+TENSOR_STEPS = (TENSOR_GROUPS * BLOCKS + 1) * BLOCK_STEPS + 5
 
 FLOPS = 2 * TOKENS * C * 2 * ROWS * D + 2 * TOKENS * ROWS * ROWS * D
 
@@ -67,11 +76,12 @@ def tile_differentialattention_pa_t_kernel(tc, x, Wq, Wk, lq1, lq2, lk1, lk2, ou
     out_rows = out.rearrange("b n a h -> (b n) (a h)")
 
     with (
+        tc.manual_schedule(),
         tc.tile_pool(name="keep", bufs=1) as keep,
         tc.tile_pool(name="stage", bufs=2) as stage,
         tc.tile_pool(name="tensor_way", bufs=1) as tensor_way,
         tc.tile_pool(name="vector_way", bufs=2) as vector_way,
-        tc.tile_pool(name="products", bufs=8) as products,
+        tc.tile_pool(name="products", bufs=LAG + 2) as products,
         tc.psum_pool(name="psum_t", bufs=2) as psum_t,
         tc.psum_pool(name="psum_y", bufs=2) as psum_y,
         tc.psum_pool(name="psum_s", bufs=2) as psum_s,
@@ -89,38 +99,29 @@ def tile_differentialattention_pa_t_kernel(tc, x, Wq, Wk, lq1, lq2, lk1, lk2, ou
         vectors = keep.tile([P, 4, D], BF16)
         for v, vec in enumerate((lq1, lq2, lk1, lk2)):
             nc.scalar.dma_start(out=vectors[:, v, :], in_=vec.partition_broadcast(P))
-        lam_products = keep.tile([P, 2, D], F32)
-        nc.vector.tensor_tensor(
-            out=lam_products[:], in0=vectors[:, 0:2, :], in1=vectors[:, 2:4, :], op=ALU.mult
-        )
-        lam_dots = keep.tile([P, 2], F32)
-        nc.vector.tensor_reduce(out=lam_dots[:], in_=lam_products[:], axis=AXIS_X, op=ALU.add)
-        lam_exps = keep.tile([P, 2], F32)
-        nc.scalar.activation(out=lam_exps[:], in_=lam_dots[:], func=ACT.Exp)
-        neg_lam = keep.tile([P, 1], F32)
-        nc.vector.tensor_tensor(
-            out=neg_lam[:], in0=lam_exps[:, 1:2], in1=lam_exps[:, 0:1], op=ALU.subtract
-        )
-        nc.vector.tensor_scalar_add(out=neg_lam[:], in0=neg_lam[:], scalar1=-LAM_INIT)
-        parity = keep.tile([P, 2], F32)
-        nc.vector.tensor_reduce(
-            out=parity[:],
-            in_=ident[:].rearrange("p (c j) -> p j c", j=2),
-            axis=AXIS_X,
-            op=ALU.add,
-        )
-        odd_neg_lam = keep.tile([P, 1], F32)
-        nc.vector.tensor_tensor(out=odd_neg_lam[:], in0=parity[:, 1:2], in1=neg_lam[:], op=ALU.mult)
-
-        w_codes = []
-        w_scales = []
-        for name, W in (("q", Wq), ("k", Wk)):
-            w_sb = stage.tile([P, HEADS * C], BF16, tag="loaded", bufs=3)
+        w_loaded = []
+        for W in (Wq, Wk):
+            w_sb = stage.tile([P, HEADS * C], BF16, tag="loaded", bufs=4)
             nc.sync.dma_start(
                 out=w_sb[:].rearrange("p (a c) -> p a c", c=C),
                 in_=W.rearrange("(a p) c -> p a c", p=P),
             )
-            w_f32 = w_sb[:].bitcast(F32)
+            w_loaded.append(w_sb)
+        x_loaded = {}
+        for g in [GROUPS - 1] + list(range(TENSOR_GROUPS)):
+            x_sb = stage.tile([P, GROUP_TILES * C], BF16, tag="loaded", bufs=4)
+            nc.sync.dma_start(
+                out=x_sb[:].rearrange("p (y c) -> p y c", c=C),
+                in_=x_rows[g * GROUP_TOKENS : (g + 1) * GROUP_TOKENS, :].rearrange(
+                    "(y p) c -> p y c", p=P
+                ),
+            )
+            x_loaded[g] = x_sb
+
+        w_codes = []
+        w_scales = []
+        for w, name in enumerate(("q", "k")):
+            w_f32 = w_loaded[w][:].bitcast(F32)
             codes = keep.tile([P, PADDED_ALL], U32, name="codes_" + name, align_bytes=64)
             scales = keep.tile([P, PADDED_ALL], U8, name="scales_" + name, align_bytes=64)
             nc.vector.memset(codes[:, PADDED:].bitcast(I32), 0)
@@ -148,42 +149,45 @@ def tile_differentialattention_pa_t_kernel(tc, x, Wq, Wk, lq1, lq2, lk1, lk2, ou
 
         x_codes = keep.tile([P, TOKENS], U32, align_bytes=64)
         x_scales = keep.tile([P, TOKENS], U8, align_bytes=64)
-        for g in [GROUPS - 1] + list(range(TENSOR_GROUPS)):
-            x_sb = stage.tile([P, GROUP_TILES * C], BF16, tag="loaded", bufs=3)
-            nc.sync.dma_start(
-                out=x_sb[:].rearrange("p (y c) -> p y c", c=C),
-                in_=x_rows[g * GROUP_TOKENS : (g + 1) * GROUP_TOKENS, :].rearrange(
-                    "(y p) c -> p y c", p=P
-                ),
-            )
-            x_f32 = x_sb[:].bitcast(F32)
-            grouped = stage.tile([P, 4 * GROUP_TOKENS], BF16, tag="grouped", align_bytes=64)
-            in_order = grouped[:].bitcast(F32).rearrange("p (w u) -> p w u", u=2)
-            by_block = grouped[:].bitcast(F32).rearrange(
-                "p (b s n t u) -> p b s n t u", b=BLOCKS, s=2, n=TILE_PAIRS, u=2
-            )
-            for n in range(TILE_PAIRS):
-                planes = transpose_words(
-                    nc, psum_t, ident, x_f32[:, 2 * n * WORDS : (2 * n + 2) * WORDS], 2
+        x_grouped = {}
+
+        def prepare_x(g, n):
+            if n == TILE_PAIRS:
+                cols = slice(g * GROUP_TOKENS, (g + 1) * GROUP_TOKENS)
+                nc.vector.quantize_mx(
+                    out=x_codes[:, cols].bitcast(FP8X4),
+                    scales=x_scales[:, cols],
+                    in_=x_grouped[g][:],
                 )
-                if g < TENSOR_GROUPS:
-                    for s in range(2):
-                        nc.scalar.copy(
-                            out=by_block[:, :, s, n],
-                            in_=planes[:, :, s * P : (s + 1) * P].rearrange(
-                                "p u (b t) -> p b t u", b=BLOCKS
-                            ),
-                        )
-                else:
-                    copy = nc.scalar.copy if n % 2 == 0 else nc.vector.tensor_copy
-                    copy(
-                        out=in_order[:, 2 * n * P : (2 * n + 2) * P, :],
-                        in_=planes[:].rearrange("p u w -> p w u"),
+                return
+            if n == 0:
+                grouped = stage.tile([P, 4 * GROUP_TOKENS], BF16, tag="grouped", align_bytes=64)
+                x_grouped[g] = grouped
+            words = x_grouped[g][:].bitcast(F32)
+            x_f32 = x_loaded[g][:].bitcast(F32)
+            planes = transpose_words(nc, psum_t, ident, x_f32[:, 2 * n * WORDS : (2 * n + 2) * WORDS], 2)
+            if g < TENSOR_GROUPS:
+                by_block = words.rearrange(
+                    "p (b s n t u) -> p b s n t u", b=BLOCKS, s=2, n=TILE_PAIRS, u=2
+                )
+                for s in range(2):
+                    nc.scalar.copy(
+                        out=by_block[:, :, s, n],
+                        in_=planes[:, :, s * P : (s + 1) * P].rearrange(
+                            "p u (b t) -> p b t u", b=BLOCKS
+                        ),
                     )
-            cols = slice(g * GROUP_TOKENS, (g + 1) * GROUP_TOKENS)
-            nc.vector.quantize_mx(
-                out=x_codes[:, cols].bitcast(FP8X4), scales=x_scales[:, cols], in_=grouped[:]
-            )
+            else:
+                in_order = words.rearrange("p (w u) -> p w u", u=2)
+                copy = nc.scalar.copy if n % 2 == 0 else nc.vector.tensor_copy
+                copy(
+                    out=in_order[:, 2 * n * P : (2 * n + 2) * P, :],
+                    in_=planes[:].rearrange("p u w -> p w u"),
+                )
+
+        for n in range(X_PIECES):
+            prepare_x(GROUPS - 1, n)
+
 
         def project_pairs(w, bank_index, first_token):
             bank = psum_y.tile([P, BANK_ROWS, P], F32, tag="y")
@@ -203,98 +207,137 @@ def tile_differentialattention_pa_t_kernel(tc, x, Wq, Wk, lq1, lq2, lk1, lk2, ou
                     )
             return bank
 
-        def score_block(g, b, diag, dense):
-            first_token = g * GROUP_TOKENS + b * BLOCK_TOKENS
-            for bank_index in range(ROWS // BANK_ROWS):
-                rows = slice(bank_index * BANK_ROWS, (bank_index + 1) * BANK_ROWS)
-                bank = project_pairs(0, bank_index, first_token)
-                for s in range(2):
-                    half = slice(s * HALF, (s + 1) * HALF)
-                    nc.scalar.copy(
-                        out=diag[half, :, :, s, rows],
-                        in_=bank[half].rearrange("p i (n t) -> p t n i", n=TILE_PAIRS),
-                    )
-            k_pairs = tensor_way.tile([P, BLOCK_T, ROWS, TILE_PAIRS], F32, bufs=2)
-            for bank_index in range(ROWS // BANK_ROWS):
-                rows = slice(bank_index * BANK_ROWS, (bank_index + 1) * BANK_ROWS)
-                bank = project_pairs(1, bank_index, first_token)
+        k_pairs = {}
+        dense = {}
+        finish = {}
+
+        def score_bank(block, bank_index):
+            g = block // BLOCKS
+            if block % BLOCKS == 0 and bank_index == 0:
+                scores = tensor_way.tile([P, P, ROWS], F32, tag="dense", bufs=2)
+                dense[g] = scores
+            t0 = bank_index * BANK_MATMULS
+            raw = psum_s.tile([P, BANK_MATMULS, SCORE_COLS], F32, tag="raw")
+            for i in range(BANK_MATMULS):
+                nc.tensor.matmul(
+                    out=raw[:, i, :],
+                    lhsT=q_diag[block % 2][:, t0 + i].rearrange("p n s r -> p (n s r)"),
+                    rhs=k_pairs[block][:, t0 + i].rearrange("p m n -> p (m n)"),
+                    start=True,
+                    stop=True,
+                )
+            first = (block % BLOCKS) * BLOCK_T + t0
+            for n in range(TILE_PAIRS):
+                quad = slice(n * QUADRANT, (n + 1) * QUADRANT)
                 nc.scalar.copy(
-                    out=k_pairs[:, :, rows, :],
-                    in_=bank[:].rearrange("p i (n t) -> p t i n", n=TILE_PAIRS),
+                    out=dense[g][quad, first : first + BANK_MATMULS, :],
+                    in_=raw[quad].rearrange("p i (m n) -> p i m n", n=TILE_PAIRS)[:, :, :, n],
                 )
-            for t0 in range(0, BLOCK_T, BANK_MATMULS):
-                raw = psum_s.tile([P, BANK_MATMULS, SCORE_COLS], F32, tag="raw")
-                for i in range(BANK_MATMULS):
-                    nc.tensor.matmul(
-                        out=raw[:, i, :],
-                        lhsT=diag[:, t0 + i].rearrange("p n s r -> p (n s r)"),
-                        rhs=k_pairs[:, t0 + i].rearrange("p m n -> p (m n)"),
-                        start=True,
-                        stop=True,
-                    )
-                for n in range(TILE_PAIRS):
-                    quad = slice(n * QUADRANT, (n + 1) * QUADRANT)
-                    first = b * BLOCK_T + t0
-                    nc.scalar.copy(
-                        out=dense[quad, first : first + BANK_MATMULS, :],
-                        in_=raw[quad].rearrange("p i (m n) -> p i m n", n=TILE_PAIRS)[:, :, :, n],
-                    )
 
-        def finish_group(g, dense):
-            dense_shape = [P, P, ROWS]
-            row_max = tensor_way.tile([P, P], F32)
-            nc.vector.tensor_reduce(out=row_max[:], in_=dense[:], axis=AXIS_X, op=ALU.max)
-            nc.vector.tensor_tensor(
-                out=dense[:],
-                in0=dense[:],
-                in1=row_max[:].unsqueeze(2).to_broadcast(dense_shape),
-                op=ALU.subtract,
-            )
-            nc.scalar.activation(out=dense[:], in_=dense[:], func=ACT.Exp, scale=SCALE)
-            row_sum = tensor_way.tile([P, P], F32)
-            nc.vector.tensor_reduce(out=row_sum[:], in_=dense[:], axis=AXIS_X, op=ALU.add)
-            inverse = tensor_way.tile([P, P], F32)
-            nc.vector.reciprocal(out=inverse[:], in_=row_sum[:])
-            by_parity = dense[:].rearrange("p t (h j) -> p j h t", j=2)
-            odd_part = tensor_way.tile([P, HEADS, P], F32)
-            nc.scalar.activation(
-                out=odd_part[:], in_=by_parity[:, 1], func=ACT.Copy, scale=odd_neg_lam[:, 0:1]
-            )
-            picked = tensor_way.tile([P, HEADS, P], F32)
-            nc.vector.scalar_tensor_tensor(
-                out=picked[:],
-                in0=by_parity[:, 0],
-                scalar=parity[:, 0:1],
-                in1=odd_part[:],
-                op0=ALU.mult,
-                op1=ALU.add,
-            )
-            nc.vector.tensor_tensor(
-                out=picked[:],
-                in0=picked[:],
-                in1=inverse[:].unsqueeze(1).to_broadcast([P, HEADS, P]),
-                op=ALU.mult,
-            )
-            result = tensor_way.tile([P, GROUP_TILES, HEADS, HEADS], F32)
-            result_rows = result[:].rearrange("p y a h -> p (y a) h")
-            for h0 in range(0, HEADS, BANK_ROWS):
-                flipped = psum_t.tile([P, BANK_ROWS, P], F32, tag="planes")
-                for i in range(BANK_ROWS):
-                    nc.tensor.transpose(flipped[:, i, :], picked[:, h0 + i, :], ident[:])
-                nc.vector.tensor_reduce(
-                    out=result_rows[:, :, h0 : h0 + BANK_ROWS],
-                    in_=flipped[:].rearrange("p i (e j) -> p e i j", j=2),
-                    axis=AXIS_X,
-                    op=ALU.add,
+        def project_bank(block, bank_index):
+            first_token = block * BLOCK_TOKENS
+            rows = slice(bank_index * BANK_ROWS, (bank_index + 1) * BANK_ROWS)
+            if bank_index == 0:
+                moving = tensor_way.tile([P, BLOCK_T, ROWS, TILE_PAIRS], F32, tag="k_pairs", bufs=2)
+                k_pairs[block] = moving
+            bank = project_pairs(0, bank_index, first_token)
+            for s in range(2):
+                half = slice(s * HALF, (s + 1) * HALF)
+                nc.scalar.copy(
+                    out=q_diag[block % 2][half, :, :, s, rows],
+                    in_=bank[half].rearrange("p i (n t) -> p t n i", n=TILE_PAIRS),
                 )
-            nc.sync.dma_start(
-                out=out_rows[g * GROUP_TOKENS : (g + 1) * GROUP_TOKENS, :].rearrange(
-                    "(y p) e -> p y e", p=P
-                ),
-                in_=result[:].rearrange("p y a h -> p y (a h)"),
+            bank = project_pairs(1, bank_index, first_token)
+            nc.scalar.copy(
+                out=k_pairs[block][:, :, rows, :],
+                in_=bank[:].rearrange("p i (n t) -> p t i n", n=TILE_PAIRS),
             )
 
-        def project_tile(w, bank_index, tok, pool, tag):
+        def finish_group(g, phase):
+            scores = dense[g]
+            by_parity = scores[:].rearrange("p t (h j) -> p j h t", j=2)
+            if phase == 0:
+                row_max = tensor_way.tile([P, P], F32)
+                nc.vector.tensor_reduce(out=row_max[:], in_=scores[:], axis=AXIS_X, op=ALU.max)
+                nc.vector.tensor_tensor(
+                    out=scores[:],
+                    in0=scores[:],
+                    in1=row_max[:].unsqueeze(2).to_broadcast([P, P, ROWS]),
+                    op=ALU.subtract,
+                )
+            if phase == 1:
+                nc.scalar.activation(out=scores[:], in_=scores[:], func=ACT.Exp, scale=SCALE)
+                odd_part = tensor_way.tile([P, HEADS, P], F32)
+                nc.scalar.activation(
+                    out=odd_part[:], in_=by_parity[:, 1], func=ACT.Copy, scale=odd_neg_lam[:, 0:1]
+                )
+                finish["odd_part"] = odd_part
+            if phase == 2:
+                row_sum = tensor_way.tile([P, P], F32)
+                nc.vector.tensor_reduce(out=row_sum[:], in_=scores[:], axis=AXIS_X, op=ALU.add)
+                inverse = tensor_way.tile([P, P], F32)
+                nc.vector.reciprocal(out=inverse[:], in_=row_sum[:])
+                picked = tensor_way.tile([P, HEADS, P], F32)
+                nc.vector.scalar_tensor_tensor(
+                    out=picked[:],
+                    in0=by_parity[:, 0],
+                    scalar=parity[:, 0:1],
+                    in1=finish["odd_part"][:],
+                    op0=ALU.mult,
+                    op1=ALU.add,
+                )
+                nc.vector.tensor_tensor(
+                    out=picked[:],
+                    in0=picked[:],
+                    in1=inverse[:].unsqueeze(1).to_broadcast([P, HEADS, P]),
+                    op=ALU.mult,
+                )
+                finish["picked"] = picked
+            if phase == 3:
+                picked = finish["picked"]
+                for half in range(2):
+                    flipped = psum_t.tile([P, BANK_ROWS, P], F32, tag="planes")
+                    for i in range(BANK_ROWS):
+                        nc.tensor.transpose(
+                            flipped[:, i, :], picked[:, half * BANK_ROWS + i, :], ident[:]
+                        )
+                    finish[half] = flipped
+            if phase == 4:
+                result = tensor_way.tile([P, GROUP_TILES, HEADS, HEADS], F32)
+                result_rows = result[:].rearrange("p y a h -> p (y a) h")
+                for half in range(2):
+                    nc.vector.tensor_reduce(
+                        out=result_rows[:, :, half * BANK_ROWS : (half + 1) * BANK_ROWS],
+                        in_=finish[half][:].rearrange("p i (e j) -> p e i j", j=2),
+                        axis=AXIS_X,
+                        op=ALU.add,
+                    )
+                nc.sync.dma_start(
+                    out=out_rows[g * GROUP_TOKENS : (g + 1) * GROUP_TOKENS, :].rearrange(
+                        "(y p) e -> p y e", p=P
+                    ),
+                    in_=result[:].rearrange("p y a h -> p y (a h)"),
+                )
+
+        def tensor_step(step):
+            block = step // BLOCK_STEPS
+            bank_index = step % BLOCK_STEPS
+            if 1 <= block <= TENSOR_GROUPS * BLOCKS:
+                score_bank(block - 1, bank_index)
+            if block < TENSOR_GROUPS * BLOCKS:
+                project_bank(block, bank_index)
+            ended = (step - BLOCK_STEPS) // GROUP_STEPS - 1
+            phase = (step - BLOCK_STEPS) % GROUP_STEPS
+            if ended >= 0 and phase < 5:
+                finish_group(ended, phase)
+            next_group = step // GROUP_STEPS + 1
+            piece = step % GROUP_STEPS - GROUP_STEPS // 2
+            if next_group < TENSOR_GROUPS and 0 <= piece < X_PIECES:
+                prepare_x(next_group, piece)
+
+        def project_tile(w, bank_index, tile_index, pool, tag):
+            first_token = (TENSOR_GROUPS * GROUP_TILES + tile_index) * P
+            tok = slice(first_token, first_token + P)
             bank = pool.tile([P, BANK], F32, tag=tag)
             w_cols = slice(D + bank_index * BANK, D + (bank_index + 1) * BANK)
             nc.tensor.matmul_mx(
@@ -308,104 +351,164 @@ def tile_differentialattention_pa_t_kernel(tc, x, Wq, Wk, lq1, lq2, lk1, lk2, ou
             )
             return bank[:].rearrange("p (i z d) -> p i z d", z=2, d=D)[:, :, 0, :]
 
-        def score_tile(tile_index, scores):
-            tok = slice(tile_index * P, (tile_index + 1) * P)
-            q_sb = vector_way.tile([P, ROWS, D], F32)
+        k_rows = {}
+        q_high = {}
+        q_low = {}
+        batches = {}
+        made = {}
+
+        def project_to_sbuf(tile_index):
             k_sb = vector_way.tile([P, ROWS, D], F32)
-            q_psum = []
+            q_sb = vector_way.tile([P, ROW_PAIRS, D], F32)
             for bank_index in range(ROWS // BANK_ROWS):
                 first = bank_index * BANK_ROWS
                 nc.scalar.copy(
                     out=k_sb[:, first : first + BANK_ROWS, :],
-                    in_=project_tile(1, bank_index, tok, psum_y, "y"),
+                    in_=project_tile(1, bank_index, tile_index, psum_y, "y"),
                 )
-                if bank_index < VECTOR_BANKS:
-                    q_bank = project_tile(0, bank_index, tok, psum_q, "q%d" % bank_index)
-                    q_psum.append(q_bank)
-                else:
-                    q_bank = project_tile(0, bank_index, tok, psum_y, "y")
-                skip = min(max(VECTOR_ROWS - first, 0), BANK_ROWS)
-                if skip < BANK_ROWS:
-                    nc.scalar.copy(
-                        out=q_sb[:, first + skip : first + BANK_ROWS, :], in_=q_bank[:, skip:, :]
-                    )
-            row_shape = [P, ROWS, D]
-            for r in range(ROWS):
-                prod = products.tile(row_shape, F32)
-                if r < VECTOR_ROWS:
-                    q_row = q_psum[r // BANK_ROWS][:, r % BANK_ROWS : r % BANK_ROWS + 1, :]
-                    engine = nc.vector
-                else:
-                    q_row = q_sb[:, r : r + 1, :]
-                    engine = nc.gpsimd
-                engine.tensor_tensor(
-                    out=prod[:], in0=q_row.to_broadcast(row_shape), in1=k_sb[:], op=ALU.mult
+            for bank_index in range(VECTOR_BANKS):
+                first = bank_index * BANK_ROWS
+                nc.scalar.copy(
+                    out=q_sb[:, first : first + BANK_ROWS, :],
+                    in_=project_tile(0, VECTOR_BANKS + bank_index, tile_index, psum_y, "y"),
                 )
-                if r < ROWS - SCALAR_SUM_ROWS:
-                    nc.vector.tensor_reduce(
-                        out=scores[:, r, :], in_=prod[:], axis=AXIS_X, op=ALU.add
-                    )
-                else:
-                    for m in range(ROWS):
-                        nc.scalar.activation(
-                            out=prod[:, m, :],
-                            in_=prod[:, m, :],
-                            func=ACT.Copy,
-                            accum_out=scores[:, r, m : m + 1],
-                        )
+            k_rows[tile_index] = k_sb
+            q_high[tile_index] = q_sb
 
-        def finish_batch(first_tile, batch):
-            batch_rows = BATCH_TILES * ROWS
-            batch_shape = [P, batch_rows, ROWS]
-            row_max = vector_way.tile([P, batch_rows], F32)
-            nc.vector.tensor_reduce(out=row_max[:], in_=batch[:], axis=AXIS_X, op=ALU.max)
+        def project_to_psum(tile_index):
+            q_low[tile_index] = [
+                project_tile(0, bank_index, tile_index, psum_q, "q%d" % bank_index)
+                for bank_index in range(VECTOR_BANKS)
+            ]
+
+        def make_products(pair):
+            tile_index = pair // ROW_PAIRS
+            j = pair % ROW_PAIRS
+            row_shape = [P, ROWS, D]
+            by_vector = products.tile(row_shape, F32, bufs=LAG + 4)
             nc.vector.tensor_tensor(
-                out=batch[:],
-                in0=batch[:],
-                in1=row_max[:].unsqueeze(2).to_broadcast(batch_shape),
-                op=ALU.subtract,
-            )
-            nc.scalar.activation(out=batch[:], in_=batch[:], func=ACT.Exp, scale=SCALE)
-            row_sum = vector_way.tile([P, batch_rows], F32)
-            nc.vector.tensor_reduce(out=row_sum[:], in_=batch[:], axis=AXIS_X, op=ALU.add)
-            factor = vector_way.tile([P, batch_rows], F32)
-            nc.vector.reciprocal(out=factor[:], in_=row_sum[:])
-            odd_rows = factor[:].rearrange("p (e j) -> p e j", j=2)[:, :, 1]
-            nc.vector.tensor_scalar_mul(out=odd_rows, in0=odd_rows, scalar1=neg_lam[:, 0:1])
-            nc.vector.tensor_tensor(
-                out=batch[:],
-                in0=batch[:],
-                in1=factor[:].unsqueeze(2).to_broadcast(batch_shape),
+                out=by_vector[:],
+                in0=q_low[tile_index][j // BANK_ROWS][
+                    :, j % BANK_ROWS : j % BANK_ROWS + 1, :
+                ].to_broadcast(row_shape),
+                in1=k_rows[tile_index][:],
                 op=ALU.mult,
             )
-            by_parity = batch[:].rearrange("p (e j) (h i) -> p e j h i", j=2, i=2)
-            result = vector_way.tile([P, BATCH_TILES * HEADS, HEADS], F32)
-            nc.vector.tensor_tensor(
-                out=result[:], in0=by_parity[:, :, 0, :, 0], in1=by_parity[:, :, 1, :, 1], op=ALU.add
+            by_gpsimd = products.tile(row_shape, F32)
+            nc.gpsimd.tensor_tensor(
+                out=by_gpsimd[:],
+                in0=q_high[tile_index][:, j : j + 1, :].to_broadcast(row_shape),
+                in1=k_rows[tile_index][:],
+                op=ALU.mult,
             )
-            nc.sync.dma_start(
-                out=out_rows[first_tile * P : (first_tile + BATCH_TILES) * P, :].rearrange(
-                    "(y p) e -> p y e", p=P
-                ),
-                in_=result[:].rearrange("p (y a) h -> p y (a h)", a=HEADS),
-            )
+            made[pair] = (by_vector, by_gpsimd)
 
-        vector_tile = 0
-        for step in range(TENSOR_GROUPS * BLOCKS):
-            g = step // BLOCKS
-            b = step % BLOCKS
-            if step % 3 < 2:
-                if vector_tile % BATCH_TILES == 0:
-                    batch = vector_way.tile([P, BATCH_TILES * ROWS, ROWS], F32)
-                i = vector_tile % BATCH_TILES
-                score_tile(
-                    TENSOR_GROUPS * GROUP_TILES + vector_tile, batch[:, i * ROWS : (i + 1) * ROWS, :]
+        def sum_products(pair):
+            tile_index = pair // ROW_PAIRS
+            j = pair % ROW_PAIRS
+            if pair % BATCH_PAIRS == 0:
+                batch = vector_way.tile([P, BATCH_TILES * ROWS, ROWS], F32)
+                batches[pair // BATCH_PAIRS] = batch
+            first_row = (tile_index % BATCH_TILES) * ROWS
+            scores = batches[pair // BATCH_PAIRS][:, first_row : first_row + ROWS, :]
+            by_vector, by_gpsimd = made[pair]
+            nc.vector.tensor_reduce(
+                out=scores[:, ROW_PAIRS + j, :], in_=by_gpsimd[:], axis=AXIS_X, op=ALU.add
+            )
+            if j < SCALAR_SUMS:
+                for m in range(ROWS):
+                    nc.scalar.activation(
+                        out=by_vector[:, m, :],
+                        in_=by_vector[:, m, :],
+                        func=ACT.Copy,
+                        accum_out=scores[:, j, m : m + 1],
+                    )
+            else:
+                nc.vector.tensor_reduce(out=scores[:, j, :], in_=by_vector[:], axis=AXIS_X, op=ALU.add)
+
+        def finish_batch(index, phase):
+            batch = batches[index]
+            batch_rows = BATCH_TILES * ROWS
+            batch_shape = [P, batch_rows, ROWS]
+            if phase == 0:
+                row_max = vector_way.tile([P, batch_rows], F32)
+                nc.vector.tensor_reduce(out=row_max[:], in_=batch[:], axis=AXIS_X, op=ALU.max)
+                nc.vector.tensor_tensor(
+                    out=batch[:],
+                    in0=batch[:],
+                    in1=row_max[:].unsqueeze(2).to_broadcast(batch_shape),
+                    op=ALU.subtract,
                 )
-                vector_tile += 1
-                if vector_tile % BATCH_TILES == 0:
-                    finish_batch(TENSOR_GROUPS * GROUP_TILES + vector_tile - BATCH_TILES, batch)
-            if b == 0:
-                dense = tensor_way.tile([P, P, ROWS], F32, bufs=2)
-            score_block(g, b, q_diag[step % 2], dense)
-            if b == BLOCKS - 1:
-                finish_group(g, dense)
+            if phase == 1:
+                nc.scalar.activation(out=batch[:], in_=batch[:], func=ACT.Exp, scale=SCALE)
+            if phase == 2:
+                row_sum = vector_way.tile([P, batch_rows], F32)
+                nc.vector.tensor_reduce(out=row_sum[:], in_=batch[:], axis=AXIS_X, op=ALU.add)
+                factor = vector_way.tile([P, batch_rows], F32)
+                nc.vector.reciprocal(out=factor[:], in_=row_sum[:])
+                odd_rows = factor[:].rearrange("p (e j) -> p e j", j=2)[:, :, 1]
+                nc.vector.tensor_scalar_mul(out=odd_rows, in0=odd_rows, scalar1=neg_lam[:, 0:1])
+                nc.vector.tensor_tensor(
+                    out=batch[:],
+                    in0=batch[:],
+                    in1=factor[:].unsqueeze(2).to_broadcast(batch_shape),
+                    op=ALU.mult,
+                )
+                by_parity = batch[:].rearrange("p (e j) (h i) -> p e j h i", j=2, i=2)
+                result = vector_way.tile([P, BATCH_TILES * HEADS, HEADS], F32)
+                nc.vector.tensor_tensor(
+                    out=result[:],
+                    in0=by_parity[:, :, 0, :, 0],
+                    in1=by_parity[:, :, 1, :, 1],
+                    op=ALU.add,
+                )
+                first_token = (TENSOR_GROUPS * GROUP_TILES + index * BATCH_TILES) * P
+                nc.sync.dma_start(
+                    out=out_rows[first_token : first_token + BATCH_TILES * P, :].rearrange(
+                        "(y p) e -> p y e", p=P
+                    ),
+                    in_=result[:].rearrange("p (y a) h -> p y (a h)", a=HEADS),
+                )
+
+        project_to_sbuf(0)
+        lam_products = keep.tile([P, 2, D], F32)
+        nc.vector.tensor_tensor(
+            out=lam_products[:], in0=vectors[:, 0:2, :], in1=vectors[:, 2:4, :], op=ALU.mult
+        )
+        lam_dots = keep.tile([P, 2], F32)
+        nc.vector.tensor_reduce(out=lam_dots[:], in_=lam_products[:], axis=AXIS_X, op=ALU.add)
+        lam_exps = keep.tile([P, 2], F32)
+        nc.scalar.activation(out=lam_exps[:], in_=lam_dots[:], func=ACT.Exp)
+        neg_lam = keep.tile([P, 1], F32)
+        nc.vector.tensor_tensor(
+            out=neg_lam[:], in0=lam_exps[:, 1:2], in1=lam_exps[:, 0:1], op=ALU.subtract
+        )
+        nc.vector.tensor_scalar_add(out=neg_lam[:], in0=neg_lam[:], scalar1=-LAM_INIT)
+        parity = keep.tile([P, 2], F32)
+        nc.vector.tensor_reduce(
+            out=parity[:],
+            in_=ident[:].rearrange("p (c j) -> p j c", j=2),
+            axis=AXIS_X,
+            op=ALU.add,
+        )
+        odd_neg_lam = keep.tile([P, 1], F32)
+        nc.vector.tensor_tensor(out=odd_neg_lam[:], in0=parity[:, 1:2], in1=neg_lam[:], op=ALU.mult)
+
+        for turn in range(ALL_PAIRS + LAG + 3):
+            if turn < X_PIECES:
+                prepare_x(0, turn)
+            elif turn - X_PIECES < TENSOR_STEPS:
+                tensor_step(turn - X_PIECES)
+            if turn < ALL_PAIRS:
+                tile_index = turn // ROW_PAIRS
+                if turn % ROW_PAIRS == 0:
+                    project_to_psum(tile_index)
+                if turn % ROW_PAIRS == ROW_PAIRS // 2 and tile_index + 1 < VECTOR_TILES:
+                    project_to_sbuf(tile_index + 1)
+            summed = turn - LAG
+            if 0 <= summed < ALL_PAIRS:
+                sum_products(summed)
+            if turn < ALL_PAIRS:
+                make_products(turn)
+            if summed >= BATCH_PAIRS and summed % BATCH_PAIRS < 3:
+                finish_batch(summed // BATCH_PAIRS - 1, summed % BATCH_PAIRS)

import math

import concourse.mybir as mybir
from concourse.masks import make_identity

F32 = mybir.dt.float32
BF16 = mybir.dt.bfloat16
I32 = mybir.dt.int32
U32 = mybir.dt.uint32
U8 = mybir.dt.uint8
FP8X4 = mybir.dt.float8_e4m3fn_x4
ALU = mybir.AluOpType
ACT = mybir.ActivationFunctionType
AXIS_X = mybir.AxisListType.X

P = 128
HALF = P // 2
QUADRANT = 32
TOKENS = 4 * 1024
C = 512
WORDS = C // 2
ROWS = 16
D = 64
HEADS = 8
BANK = 512
BANK_ROWS = 4
SCALE = D ** -0.5
LAM_INIT = 0.8 - 0.6 * math.exp(-0.3 * 12)

GROUP_TILES = 8
GROUP_TOKENS = GROUP_TILES * P
GROUPS = TOKENS // GROUP_TOKENS
TENSOR_GROUPS = 3
TILE_PAIRS = GROUP_TILES // 2
BLOCKS = 4
BLOCK_T = P // BLOCKS
BLOCK_TOKENS = GROUP_TILES * BLOCK_T
X_PIECES = TILE_PAIRS + 1
SCORE_COLS = ROWS * TILE_PAIRS
BANK_MATMULS = BANK // SCORE_COLS

PADDED = 2 * ROWS * D
PADDED_ALL = PADDED + D

VECTOR_TILES = GROUP_TILES
ROW_PAIRS = ROWS // 2
ALL_PAIRS = VECTOR_TILES * ROW_PAIRS
VECTOR_BANKS = ROW_PAIRS // BANK_ROWS
SCALAR_SUMS = 3
LAG = 2
BATCH_TILES = 2
BATCH_PAIRS = BATCH_TILES * ROW_PAIRS

BLOCK_STEPS = ROWS // BANK_ROWS
GROUP_STEPS = BLOCKS * BLOCK_STEPS
TENSOR_STEPS = (TENSOR_GROUPS * BLOCKS + 1) * BLOCK_STEPS + 5

FLOPS = 2 * TOKENS * C * 2 * ROWS * D + 2 * TOKENS * ROWS * ROWS * D


def transpose_words(nc, psum, ident, rows_f32, blocks):
    planes = psum.tile([P, 2, blocks * P], F32, tag="planes")
    for b in range(blocks):
        for u in range(2):
            nc.tensor.transpose(
                planes[:, u, b * P : (b + 1) * P],
                rows_f32[:, b * WORDS + u * P : b * WORDS + (u + 1) * P],
                ident[:],
            )
    return planes


def tile_differentialattention_pa_t_kernel(tc, x, Wq, Wk, lq1, lq2, lk1, lk2, out):
    nc = tc.nc
    x_rows = x.flatten_outer_dims()
    out_rows = out.rearrange("b n a h -> (b n) (a h)")

    with (
        tc.manual_schedule(),
        tc.tile_pool(name="keep", bufs=1) as keep,
        tc.tile_pool(name="stage", bufs=2) as stage,
        tc.tile_pool(name="tensor_way", bufs=1) as tensor_way,
        tc.tile_pool(name="vector_way", bufs=2) as vector_way,
        tc.tile_pool(name="products", bufs=LAG + 2) as products,
        tc.psum_pool(name="psum_t", bufs=2) as psum_t,
        tc.psum_pool(name="psum_y", bufs=2) as psum_y,
        tc.psum_pool(name="psum_s", bufs=2) as psum_s,
        tc.psum_pool(name="psum_q", bufs=1) as psum_q,
    ):
        ident = keep.tile([P, P], F32)
        make_identity(nc, ident[:])

        q_diag = []
        for turn in range(2):
            diag = keep.tile([P, BLOCK_T, TILE_PAIRS, 2, ROWS], F32, name="q_diag%d" % turn)
            nc.gpsimd.memset(diag[:], 0.0)
            q_diag.append(diag)

        vectors = keep.tile([P, 4, D], BF16)
        for v, vec in enumerate((lq1, lq2, lk1, lk2)):
            nc.scalar.dma_start(out=vectors[:, v, :], in_=vec.partition_broadcast(P))
        w_loaded = []
        for W in (Wq, Wk):
            w_sb = stage.tile([P, HEADS * C], BF16, tag="loaded", bufs=4)
            nc.sync.dma_start(
                out=w_sb[:].rearrange("p (a c) -> p a c", c=C),
                in_=W.rearrange("(a p) c -> p a c", p=P),
            )
            w_loaded.append(w_sb)
        x_loaded = {}
        for g in [GROUPS - 1] + list(range(TENSOR_GROUPS)):
            x_sb = stage.tile([P, GROUP_TILES * C], BF16, tag="loaded", bufs=4)
            nc.sync.dma_start(
                out=x_sb[:].rearrange("p (y c) -> p y c", c=C),
                in_=x_rows[g * GROUP_TOKENS : (g + 1) * GROUP_TOKENS, :].rearrange(
                    "(y p) c -> p y c", p=P
                ),
            )
            x_loaded[g] = x_sb

        w_codes = []
        w_scales = []
        for w, name in enumerate(("q", "k")):
            w_f32 = w_loaded[w][:].bitcast(F32)
            codes = keep.tile([P, PADDED_ALL], U32, name="codes_" + name, align_bytes=64)
            scales = keep.tile([P, PADDED_ALL], U8, name="scales_" + name, align_bytes=64)
            nc.vector.memset(codes[:, PADDED:].bitcast(I32), 0)
            nc.vector.memset(scales[:, PADDED:].bitcast(I32), 0)
            for part in range(2):
                grouped = stage.tile([P, 4 * PADDED // 2], BF16, tag="grouped", align_bytes=64)
                grouped_words = grouped[:].bitcast(F32)
                nc.vector.memset(grouped_words, 0.0)
                by_row = grouped_words.rearrange(
                    "p (a j z d u) -> p a j z d u", a=HEADS // 2, j=2, z=2, d=D
                )
                for a0 in range(0, HEADS // 2, 2):
                    first = (part * (HEADS // 2) + a0) * WORDS
                    planes = transpose_words(nc, psum_t, ident, w_f32[:, first : first + 2 * WORDS], 2)
                    by_j = planes[:].rearrange("p u (a d j) -> p j a d u", a=2, j=2)
                    copy = nc.scalar.copy if a0 == 0 else nc.vector.tensor_copy
                    for j in range(2):
                        copy(out=by_row[:, a0 : a0 + 2, j, 1], in_=by_j[:, j])
                cols = slice(part * PADDED // 2, (part + 1) * PADDED // 2)
                nc.vector.quantize_mx(
                    out=codes[:, cols].bitcast(FP8X4), scales=scales[:, cols], in_=grouped[:]
                )
            w_codes.append(codes)
            w_scales.append(scales)

        x_codes = keep.tile([P, TOKENS], U32, align_bytes=64)
        x_scales = keep.tile([P, TOKENS], U8, align_bytes=64)
        x_grouped = {}

        def prepare_x(g, n):
            if n == TILE_PAIRS:
                cols = slice(g * GROUP_TOKENS, (g + 1) * GROUP_TOKENS)
                nc.vector.quantize_mx(
                    out=x_codes[:, cols].bitcast(FP8X4),
                    scales=x_scales[:, cols],
                    in_=x_grouped[g][:],
                )
                return
            if n == 0:
                grouped = stage.tile([P, 4 * GROUP_TOKENS], BF16, tag="grouped", align_bytes=64)
                x_grouped[g] = grouped
            words = x_grouped[g][:].bitcast(F32)
            x_f32 = x_loaded[g][:].bitcast(F32)
            planes = transpose_words(nc, psum_t, ident, x_f32[:, 2 * n * WORDS : (2 * n + 2) * WORDS], 2)
            if g < TENSOR_GROUPS:
                by_block = words.rearrange(
                    "p (b s n t u) -> p b s n t u", b=BLOCKS, s=2, n=TILE_PAIRS, u=2
                )
                for s in range(2):
                    nc.scalar.copy(
                        out=by_block[:, :, s, n],
                        in_=planes[:, :, s * P : (s + 1) * P].rearrange(
                            "p u (b t) -> p b t u", b=BLOCKS
                        ),
                    )
            else:
                in_order = words.rearrange("p (w u) -> p w u", u=2)
                copy = nc.scalar.copy if n % 2 == 0 else nc.vector.tensor_copy
                copy(
                    out=in_order[:, 2 * n * P : (2 * n + 2) * P, :],
                    in_=planes[:].rearrange("p u w -> p w u"),
                )

        for n in range(X_PIECES):
            prepare_x(GROUPS - 1, n)


        def project_pairs(w, bank_index, first_token):
            bank = psum_y.tile([P, BANK_ROWS, P], F32, tag="y")
            for i in range(BANK_ROWS):
                r = bank_index * BANK_ROWS + i
                for s in range(2):
                    w_cols = slice(P * r + D * (1 - s), P * r + D * (1 - s) + P)
                    x_cols = slice(first_token + s * P, first_token + (s + 1) * P)
                    nc.tensor.matmul_mx(
                        out=bank[:, i, :],
                        lhsT=w_codes[w][:, w_cols].bitcast(FP8X4),
                        lhsT_scale=w_scales[w][:, w_cols],
                        rhs=x_codes[:, x_cols].bitcast(FP8X4),
                        rhs_scale=x_scales[:, x_cols],
                        start=(s == 0),
                        stop=(s == 1),
                    )
            return bank

        k_pairs = {}
        dense = {}
        finish = {}

        def score_bank(block, bank_index):
            g = block // BLOCKS
            if block % BLOCKS == 0 and bank_index == 0:
                scores = tensor_way.tile([P, P, ROWS], F32, tag="dense", bufs=2)
                dense[g] = scores
            t0 = bank_index * BANK_MATMULS
            raw = psum_s.tile([P, BANK_MATMULS, SCORE_COLS], F32, tag="raw")
            for i in range(BANK_MATMULS):
                nc.tensor.matmul(
                    out=raw[:, i, :],
                    lhsT=q_diag[block % 2][:, t0 + i].rearrange("p n s r -> p (n s r)"),
                    rhs=k_pairs[block][:, t0 + i].rearrange("p m n -> p (m n)"),
                    start=True,
                    stop=True,
                )
            first = (block % BLOCKS) * BLOCK_T + t0
            for n in range(TILE_PAIRS):
                quad = slice(n * QUADRANT, (n + 1) * QUADRANT)
                nc.scalar.copy(
                    out=dense[g][quad, first : first + BANK_MATMULS, :],
                    in_=raw[quad].rearrange("p i (m n) -> p i m n", n=TILE_PAIRS)[:, :, :, n],
                )

        def project_bank(block, bank_index):
            first_token = block * BLOCK_TOKENS
            rows = slice(bank_index * BANK_ROWS, (bank_index + 1) * BANK_ROWS)
            if bank_index == 0:
                moving = tensor_way.tile([P, BLOCK_T, ROWS, TILE_PAIRS], F32, tag="k_pairs", bufs=2)
                k_pairs[block] = moving
            bank = project_pairs(0, bank_index, first_token)
            for s in range(2):
                half = slice(s * HALF, (s + 1) * HALF)
                nc.scalar.copy(
                    out=q_diag[block % 2][half, :, :, s, rows],
                    in_=bank[half].rearrange("p i (n t) -> p t n i", n=TILE_PAIRS),
                )
            bank = project_pairs(1, bank_index, first_token)
            nc.scalar.copy(
                out=k_pairs[block][:, :, rows, :],
                in_=bank[:].rearrange("p i (n t) -> p t i n", n=TILE_PAIRS),
            )

        def finish_group(g, phase):
            scores = dense[g]
            by_parity = scores[:].rearrange("p t (h j) -> p j h t", j=2)
            if phase == 0:
                row_max = tensor_way.tile([P, P], F32)
                nc.vector.tensor_reduce(out=row_max[:], in_=scores[:], axis=AXIS_X, op=ALU.max)
                nc.vector.tensor_tensor(
                    out=scores[:],
                    in0=scores[:],
                    in1=row_max[:].unsqueeze(2).to_broadcast([P, P, ROWS]),
                    op=ALU.subtract,
                )
            if phase == 1:
                nc.scalar.activation(out=scores[:], in_=scores[:], func=ACT.Exp, scale=SCALE)
                odd_part = tensor_way.tile([P, HEADS, P], F32)
                nc.scalar.activation(
                    out=odd_part[:], in_=by_parity[:, 1], func=ACT.Copy, scale=odd_neg_lam[:, 0:1]
                )
                finish["odd_part"] = odd_part
            if phase == 2:
                row_sum = tensor_way.tile([P, P], F32)
                nc.vector.tensor_reduce(out=row_sum[:], in_=scores[:], axis=AXIS_X, op=ALU.add)
                inverse = tensor_way.tile([P, P], F32)
                nc.vector.reciprocal(out=inverse[:], in_=row_sum[:])
                picked = tensor_way.tile([P, HEADS, P], F32)
                nc.vector.scalar_tensor_tensor(
                    out=picked[:],
                    in0=by_parity[:, 0],
                    scalar=parity[:, 0:1],
                    in1=finish["odd_part"][:],
                    op0=ALU.mult,
                    op1=ALU.add,
                )
                nc.vector.tensor_tensor(
                    out=picked[:],
                    in0=picked[:],
                    in1=inverse[:].unsqueeze(1).to_broadcast([P, HEADS, P]),
                    op=ALU.mult,
                )
                finish["picked"] = picked
            if phase == 3:
                picked = finish["picked"]
                for half in range(2):
                    flipped = psum_t.tile([P, BANK_ROWS, P], F32, tag="planes")
                    for i in range(BANK_ROWS):
                        nc.tensor.transpose(
                            flipped[:, i, :], picked[:, half * BANK_ROWS + i, :], ident[:]
                        )
                    finish[half] = flipped
            if phase == 4:
                result = tensor_way.tile([P, GROUP_TILES, HEADS, HEADS], F32)
                result_rows = result[:].rearrange("p y a h -> p (y a) h")
                for half in range(2):
                    nc.vector.tensor_reduce(
                        out=result_rows[:, :, half * BANK_ROWS : (half + 1) * BANK_ROWS],
                        in_=finish[half][:].rearrange("p i (e j) -> p e i j", j=2),
                        axis=AXIS_X,
                        op=ALU.add,
                    )
                nc.sync.dma_start(
                    out=out_rows[g * GROUP_TOKENS : (g + 1) * GROUP_TOKENS, :].rearrange(
                        "(y p) e -> p y e", p=P
                    ),
                    in_=result[:].rearrange("p y a h -> p y (a h)"),
                )

        def tensor_step(step):
            block = step // BLOCK_STEPS
            bank_index = step % BLOCK_STEPS
            if 1 <= block <= TENSOR_GROUPS * BLOCKS:
                score_bank(block - 1, bank_index)
            if block < TENSOR_GROUPS * BLOCKS:
                project_bank(block, bank_index)
            ended = (step - BLOCK_STEPS) // GROUP_STEPS - 1
            phase = (step - BLOCK_STEPS) % GROUP_STEPS
            if ended >= 0 and phase < 5:
                finish_group(ended, phase)
            next_group = step // GROUP_STEPS + 1
            piece = step % GROUP_STEPS - GROUP_STEPS // 2
            if next_group < TENSOR_GROUPS and 0 <= piece < X_PIECES:
                prepare_x(next_group, piece)

        def project_tile(w, bank_index, tile_index, pool, tag):
            first_token = (TENSOR_GROUPS * GROUP_TILES + tile_index) * P
            tok = slice(first_token, first_token + P)
            bank = pool.tile([P, BANK], F32, tag=tag)
            w_cols = slice(D + bank_index * BANK, D + (bank_index + 1) * BANK)
            nc.tensor.matmul_mx(
                out=bank[:],
                lhsT=x_codes[:, tok].bitcast(FP8X4),
                lhsT_scale=x_scales[:, tok],
                rhs=w_codes[w][:, w_cols].bitcast(FP8X4),
                rhs_scale=w_scales[w][:, w_cols],
                start=True,
                stop=True,
            )
            return bank[:].rearrange("p (i z d) -> p i z d", z=2, d=D)[:, :, 0, :]

        k_rows = {}
        q_high = {}
        q_low = {}
        batches = {}
        made = {}

        def project_to_sbuf(tile_index):
            k_sb = vector_way.tile([P, ROWS, D], F32)
            q_sb = vector_way.tile([P, ROW_PAIRS, D], F32)
            for bank_index in range(ROWS // BANK_ROWS):
                first = bank_index * BANK_ROWS
                nc.scalar.copy(
                    out=k_sb[:, first : first + BANK_ROWS, :],
                    in_=project_tile(1, bank_index, tile_index, psum_y, "y"),
                )
            for bank_index in range(VECTOR_BANKS):
                first = bank_index * BANK_ROWS
                nc.scalar.copy(
                    out=q_sb[:, first : first + BANK_ROWS, :],
                    in_=project_tile(0, VECTOR_BANKS + bank_index, tile_index, psum_y, "y"),
                )
            k_rows[tile_index] = k_sb
            q_high[tile_index] = q_sb

        def project_to_psum(tile_index):
            q_low[tile_index] = [
                project_tile(0, bank_index, tile_index, psum_q, "q%d" % bank_index)
                for bank_index in range(VECTOR_BANKS)
            ]

        def make_products(pair):
            tile_index = pair // ROW_PAIRS
            j = pair % ROW_PAIRS
            row_shape = [P, ROWS, D]
            by_vector = products.tile(row_shape, F32, bufs=LAG + 4)
            nc.vector.tensor_tensor(
                out=by_vector[:],
                in0=q_low[tile_index][j // BANK_ROWS][
                    :, j % BANK_ROWS : j % BANK_ROWS + 1, :
                ].to_broadcast(row_shape),
                in1=k_rows[tile_index][:],
                op=ALU.mult,
            )
            by_gpsimd = products.tile(row_shape, F32)
            nc.gpsimd.tensor_tensor(
                out=by_gpsimd[:],
                in0=q_high[tile_index][:, j : j + 1, :].to_broadcast(row_shape),
                in1=k_rows[tile_index][:],
                op=ALU.mult,
            )
            made[pair] = (by_vector, by_gpsimd)

        def sum_products(pair):
            tile_index = pair // ROW_PAIRS
            j = pair % ROW_PAIRS
            if pair % BATCH_PAIRS == 0:
                batch = vector_way.tile([P, BATCH_TILES * ROWS, ROWS], F32)
                batches[pair // BATCH_PAIRS] = batch
            first_row = (tile_index % BATCH_TILES) * ROWS
            scores = batches[pair // BATCH_PAIRS][:, first_row : first_row + ROWS, :]
            by_vector, by_gpsimd = made[pair]
            nc.vector.tensor_reduce(
                out=scores[:, ROW_PAIRS + j, :], in_=by_gpsimd[:], axis=AXIS_X, op=ALU.add
            )
            if j < SCALAR_SUMS:
                for m in range(ROWS):
                    nc.scalar.activation(
                        out=by_vector[:, m, :],
                        in_=by_vector[:, m, :],
                        func=ACT.Copy,
                        accum_out=scores[:, j, m : m + 1],
                    )
            else:
                nc.vector.tensor_reduce(out=scores[:, j, :], in_=by_vector[:], axis=AXIS_X, op=ALU.add)

        def finish_batch(index, phase):
            batch = batches[index]
            batch_rows = BATCH_TILES * ROWS
            batch_shape = [P, batch_rows, ROWS]
            if phase == 0:
                row_max = vector_way.tile([P, batch_rows], F32)
                nc.vector.tensor_reduce(out=row_max[:], in_=batch[:], axis=AXIS_X, op=ALU.max)
                nc.vector.tensor_tensor(
                    out=batch[:],
                    in0=batch[:],
                    in1=row_max[:].unsqueeze(2).to_broadcast(batch_shape),
                    op=ALU.subtract,
                )
            if phase == 1:
                nc.scalar.activation(out=batch[:], in_=batch[:], func=ACT.Exp, scale=SCALE)
            if phase == 2:
                row_sum = vector_way.tile([P, batch_rows], F32)
                nc.vector.tensor_reduce(out=row_sum[:], in_=batch[:], axis=AXIS_X, op=ALU.add)
                factor = vector_way.tile([P, batch_rows], F32)
                nc.vector.reciprocal(out=factor[:], in_=row_sum[:])
                odd_rows = factor[:].rearrange("p (e j) -> p e j", j=2)[:, :, 1]
                nc.vector.tensor_scalar_mul(out=odd_rows, in0=odd_rows, scalar1=neg_lam[:, 0:1])
                nc.vector.tensor_tensor(
                    out=batch[:],
                    in0=batch[:],
                    in1=factor[:].unsqueeze(2).to_broadcast(batch_shape),
                    op=ALU.mult,
                )
                by_parity = batch[:].rearrange("p (e j) (h i) -> p e j h i", j=2, i=2)
                result = vector_way.tile([P, BATCH_TILES * HEADS, HEADS], F32)
                nc.vector.tensor_tensor(
                    out=result[:],
                    in0=by_parity[:, :, 0, :, 0],
                    in1=by_parity[:, :, 1, :, 1],
                    op=ALU.add,
                )
                first_token = (TENSOR_GROUPS * GROUP_TILES + index * BATCH_TILES) * P
                nc.sync.dma_start(
                    out=out_rows[first_token : first_token + BATCH_TILES * P, :].rearrange(
                        "(y p) e -> p y e", p=P
                    ),
                    in_=result[:].rearrange("p (y a) h -> p y (a h)", a=HEADS),
                )

        project_to_sbuf(0)
        lam_products = keep.tile([P, 2, D], F32)
        nc.vector.tensor_tensor(
            out=lam_products[:], in0=vectors[:, 0:2, :], in1=vectors[:, 2:4, :], op=ALU.mult
        )
        lam_dots = keep.tile([P, 2], F32)
        nc.vector.tensor_reduce(out=lam_dots[:], in_=lam_products[:], axis=AXIS_X, op=ALU.add)
        lam_exps = keep.tile([P, 2], F32)
        nc.scalar.activation(out=lam_exps[:], in_=lam_dots[:], func=ACT.Exp)
        neg_lam = keep.tile([P, 1], F32)
        nc.vector.tensor_tensor(
            out=neg_lam[:], in0=lam_exps[:, 1:2], in1=lam_exps[:, 0:1], op=ALU.subtract
        )
        nc.vector.tensor_scalar_add(out=neg_lam[:], in0=neg_lam[:], scalar1=-LAM_INIT)
        parity = keep.tile([P, 2], F32)
        nc.vector.tensor_reduce(
            out=parity[:],
            in_=ident[:].rearrange("p (c j) -> p j c", j=2),
            axis=AXIS_X,
            op=ALU.add,
        )
        odd_neg_lam = keep.tile([P, 1], F32)
        nc.vector.tensor_tensor(out=odd_neg_lam[:], in0=parity[:, 1:2], in1=neg_lam[:], op=ALU.mult)

        for turn in range(ALL_PAIRS + LAG + 3):
            if turn < X_PIECES:
                prepare_x(0, turn)
            elif turn - X_PIECES < TENSOR_STEPS:
                tensor_step(turn - X_PIECES)
            if turn < ALL_PAIRS:
                tile_index = turn // ROW_PAIRS
                if turn % ROW_PAIRS == 0:
                    project_to_psum(tile_index)
                if turn % ROW_PAIRS == ROW_PAIRS // 2 and tile_index + 1 < VECTOR_TILES:
                    project_to_sbuf(tile_index + 1)
            summed = turn - LAG
            if 0 <= summed < ALL_PAIRS:
                sum_products(summed)
            if turn < ALL_PAIRS:
                make_products(turn)
            if summed >= BATCH_PAIRS and summed % BATCH_PAIRS < 3:
                finish_batch(summed // BATCH_PAIRS - 1, summed % BATCH_PAIRS)
